import numpy as np
import ml_dtypes


def mxq(x, axis, fmt="e4m3"):
    dtype, down = {"e4m3": (ml_dtypes.float8_e4m3fn, 7), "e5m2": (ml_dtypes.float8_e5m2, 14)}[fmt]
    v = np.moveaxis(np.asarray(x, np.float32).astype(ml_dtypes.bfloat16).astype(np.float64), axis, -1)
    blocks = v.reshape(v.shape[:-1] + (-1, 32))
    amax = np.abs(blocks).max(-1, keepdims=True)
    byte = np.maximum(np.where(amax > 0, np.frexp(amax)[1] - 1 + 127, 0) - down, 1)
    scale = np.exp2(byte - 127.0)
    codes = (blocks / scale).astype(np.float32).astype(dtype).astype(np.float64)
    return np.moveaxis((codes * scale).reshape(v.shape), -1, axis)


WIDE = False


def mx_kscale(k):
    if not WIDE:
        return np.ones(k)
    levels = np.array([10, -10, 5, -5, 0])
    a = np.random.permutation(np.resize(levels, k // 512 * 4)).reshape(k // 512, 4)
    idx = np.arange(k)
    return np.exp2(a[idx // 512, idx % 128 // 32])


BF16 = ml_dtypes.bfloat16


def bf(x):
    return np.asarray(x, np.float32).astype(BF16)


def f64(x):
    return np.asarray(x).astype(np.float64)


B, N, E, H, G, D, WIN = 1, 1024, 1024, 8, 4, 128, 512
HK = H // G
HALF = D // 2


def apply_rope(y, cos, sin):
    By, Ny, Hy, Dy = y.shape
    yp = y.reshape(By, Ny, Hy, Dy // 2, 2)
    y0, y1 = yp[..., 0], yp[..., 1]
    c = cos[:, :, None, :]
    s = sin[:, :, None, :]
    r0 = y0 * c - y1 * s
    r1 = y0 * s + y1 * c
    return np.stack([r0, r1], axis=-1).reshape(By, Ny, Hy, Dy)


def setup_inputs():
    s = mx_kscale(E)
    inv_freq = 1.0 / 10000.0 ** (np.arange(HALF) / HALF)
    ang = np.arange(N)[:, None] * inv_freq[None, :]
    return {"x": bf(np.random.standard_normal((B, N, E)) * s),
            "rope_cos": bf(np.broadcast_to(np.cos(ang)[None], (B, N, HALF))),
            "rope_sin": bf(np.broadcast_to(np.sin(ang)[None], (B, N, HALF))),
            "Wq": bf(np.random.standard_normal((E, H * D)) * 1.5 / np.sqrt(E) / s[:, None]),
            "Wk": bf(np.random.standard_normal((E, HK * D)) * 1.5 / np.sqrt(E) / s[:, None]),
            "Wv": bf(np.random.standard_normal((E, HK * D)) / np.sqrt(E) / s[:, None])}


def reference(x, rope_cos, rope_sin, Wq, Wk, Wv):
    xq = mxq(f64(x), 2, "e4m3")
    q = (xq @ mxq(f64(Wq), 0, "e4m3")).reshape(B, N, H, D)
    k = (xq @ mxq(f64(Wk), 0, "e4m3")).reshape(B, N, HK, D)
    v = (xq @ mxq(f64(Wv), 0, "e4m3")).reshape(B, N, HK, D)
    q = apply_rope(q, f64(rope_cos), f64(rope_sin))
    k = apply_rope(k, f64(rope_cos), f64(rope_sin))
    return q.transpose(0, 2, 1, 3), k.transpose(0, 2, 1, 3), v.transpose(0, 2, 1, 3)

@@ -1,0 +1,235 @@
+from contextlib import ExitStack
+
+import concourse.mybir as mybir
+from concourse.masks import make_identity
+
+F32 = mybir.dt.float32
+BF16 = mybir.dt.bfloat16
+U32 = mybir.dt.uint32
+U8 = mybir.dt.uint8
+FP8X4 = mybir.dt.float8_e4m3fn_x4
+MULT = mybir.AluOpType.mult
+ADD = mybir.AluOpType.add
+
+P = 128
+PACK = 4
+K_PASS = P * PACK
+TOKENS = 1024
+FEATURES = 1024
+PASSES = FEATURES // K_PASS
+TILES = TOKENS // P
+HEAD = 128
+PAIRS = HEAD // 2
+BANK = 512
+Q_HEADS = 8
+KV_HEADS = 2
+BANK_HEADS = BANK // HEAD
+Q_ROUNDS = Q_HEADS // BANK_HEADS
+ROUNDS = Q_ROUNDS + 1
+KV_COLS = KV_HEADS * HEAD
+WORDS = K_PASS // 2
+X_CHUNK = 2
+STORE_TILES = 4
+
+FLOPS = 2 * TOKENS * FEATURES * (Q_HEADS + 2 * KV_HEADS) * HEAD
+
+
+def tile_groupedqueryattention_pa_kernel(
+    tc, x, rope_cos, rope_sin, Wq, Wk, Wv, out_0, out_1, out_2
+):
+    nc = tc.nc
+    with ExitStack() as stack:
+        keep = stack.enter_context(tc.tile_pool(name="keep", bufs=1))
+        products = stack.enter_context(tc.tile_pool(name="products", bufs=4))
+        banks = stack.enter_context(tc.psum_pool(name="banks", bufs=8))
+
+        x_view = x[0].rearrange("(p t) k -> p t k", t=TILES)
+        cos_view = rope_cos[0].rearrange("(p t) i -> p t i", t=TILES)
+        sin_view = rope_sin[0].rearrange("(p t) i -> p t i", t=TILES)
+        wq_view = Wq.rearrange("(g p j) c -> g p j c", g=PASSES, j=PACK)
+        wk_view = Wk.rearrange("(g p j) c -> g p j c", g=PASSES, j=PACK)
+        wv_view = Wv.rearrange("(g p j) c -> g p j c", g=PASSES, j=PACK)
+        q_view = out_0[0].rearrange("h (p t) d -> p h t d", t=TILES)
+        k_view = out_1[0].rearrange("h (p t) d -> p h t d", t=TILES)
+        v_view = out_2[0].rearrange("h (p t) d -> p h t d", t=TILES)
+
+        identity = keep.tile([P, P], F32)
+        x_rows = keep.tile([P, TILES, FEATURES], BF16)
+        x_grouped = keep.tile([P, TILES, FEATURES], BF16, align_bytes=64)
+        x_codes = keep.tile([P, TILES, PASSES * P], U32, align_bytes=64)
+        x_scales = keep.tile([P, TILES, PASSES * P], U8, align_bytes=64)
+        w_rows = [
+            keep.tile([P, PASSES, PACK, BANK], BF16, name="w_rows%d" % r) for r in range(ROUNDS)
+        ]
+        w_grouped = [
+            keep.tile([P, PASSES, BANK, PACK], BF16, name="w_grouped%d" % r, align_bytes=64)
+            for r in range(ROUNDS)
+        ]
+        w_codes = [
+            keep.tile([P, PASSES, BANK], U32, name="w_codes%d" % r, align_bytes=64)
+            for r in range(ROUNDS)
+        ]
+        w_scales = [
+            keep.tile([P, PASSES, BANK], U8, name="w_scales%d" % r, align_bytes=64)
+            for r in range(ROUNDS)
+        ]
+        cos_rows = keep.tile([P, TILES, PAIRS], BF16)
+        sin_rows = keep.tile([P, TILES, PAIRS], BF16)
+        for_even = keep.tile([P, TILES, 2, PAIRS], F32)
+        for_odd = keep.tile([P, TILES, 2, PAIRS], F32)
+        q_rotated = [
+            keep.tile([P, BANK_HEADS, TILES, HEAD], F32, name="q_rotated%d" % r)
+            for r in range(Q_ROUNDS)
+        ]
+        k_rotated = keep.tile([P, KV_HEADS, TILES, HEAD], F32)
+        v_plain = keep.tile([P, KV_HEADS, TILES, HEAD], F32)
+
+        nc.scalar.dma_start(out=cos_rows[:], in_=cos_view)
+        nc.scalar.dma_start(out=sin_rows[:], in_=sin_view)
+
+        def load_x(chunk):
+            tiles = slice(chunk * X_CHUNK, (chunk + 1) * X_CHUNK)
+            nc.sync.dma_start(out=x_rows[:, tiles, :], in_=x_view[:, tiles, :])
+
+        def load_weights(r):
+            for g in range(PASSES):
+                if r < Q_ROUNDS:
+                    cols = slice(r * BANK, (r + 1) * BANK)
+                    nc.sync.dma_start(out=w_rows[r][:, g, :, :], in_=wq_view[g, :, :, cols])
+                else:
+                    nc.sync.dma_start(out=w_rows[r][:, g, :, 0:KV_COLS], in_=wk_view[g])
+                    nc.sync.dma_start(out=w_rows[r][:, g, :, KV_COLS:BANK], in_=wv_view[g])
+
+        load_x(0)
+        load_weights(0)
+        for chunk in range(1, TILES // X_CHUNK):
+            load_x(chunk)
+        for r in range(1, ROUNDS):
+            load_weights(r)
+
+        make_identity(nc, identity[:])
+
+        nc.scalar.copy(out=for_even[:, :, 0, :], in_=cos_rows[:])
+        nc.scalar.copy(out=for_odd[:, :, 1, :], in_=cos_rows[:])
+        nc.vector.tensor_copy(out=for_even[:, :, 1, :], in_=sin_rows[:])
+        nc.vector.tensor_scalar_mul(out=for_odd[:, :, 0, :], in0=sin_rows[:], scalar1=-1.0)
+
+        def quantise_x(t):
+            words = x_rows[:, t, :].bitcast(F32)
+            turned = banks.tile([P, BANK], F32, tag="bank")
+            for g in range(PASSES):
+                for u in range(2):
+                    first = g * WORDS + u
+                    piece = (g * 2 + u) * P
+                    nc.tensor.transpose(
+                        turned[:, piece : piece + P],
+                        words[:, first : (g + 1) * WORDS : 2],
+                        identity[:],
+                    )
+            nc.scalar.copy(
+                out=x_grouped[:, t, :].bitcast(F32).rearrange("p (g n u) -> p g n u", g=PASSES, u=2),
+                in_=turned[:].rearrange("p (g u n) -> p g n u", g=PASSES, u=2),
+            )
+            nc.vector.quantize_mx(
+                out=x_codes[:, t, :].bitcast(FP8X4),
+                scales=x_scales[:, t, :],
+                in_=x_grouped[:, t, :],
+            )
+
+        def quantise_weights(r, copy):
+            for g in range(PASSES):
+                copy(
+                    out=w_grouped[r][:, g, :, :].rearrange("p (c i) j -> p c j i", i=4),
+                    in_=w_rows[r][:, g, :, :].rearrange("p j (c i) -> p c j i", i=4),
+                )
+            for g in range(PASSES):
+                nc.vector.quantize_mx(
+                    out=w_codes[r][:, g, :].bitcast(FP8X4),
+                    scales=w_scales[r][:, g, :],
+                    in_=w_grouped[r][:, g, :, :].rearrange("p c j -> p (c j)"),
+                )
+
+        def project(sums, t, r, cols):
+            for g in range(PASSES):
+                tokens = slice(g * P, (g + 1) * P)
+                nc.tensor.matmul_mx(
+                    out=sums,
+                    lhsT=x_codes[:, t, tokens].bitcast(FP8X4),
+                    lhsT_scale=x_scales[:, t, tokens],
+                    rhs=w_codes[r][:, g, cols].bitcast(FP8X4),
+                    rhs_scale=w_scales[r][:, g, cols],
+                    start=(g == 0),
+                    stop=(g == PASSES - 1),
+                )
+
+        def rotate(bank, first_tile, tiles, heads, rotated):
+            shape = [P, tiles, heads, 2, PAIRS]
+            y = bank[:].rearrange("p (t h i e) -> p t h e i", t=tiles, h=heads, e=2)
+            span = slice(first_tile, first_tile + tiles)
+            from_even = products.tile([P, BANK], F32, tag="from_even")
+            from_odd = products.tile([P, BANK], F32, tag="from_odd")
+            nc.vector.tensor_tensor(
+                out=from_even[:].rearrange("p (t h e i) -> p t h e i", t=tiles, h=heads, e=2),
+                in0=y[:, :, :, 0:1, :].to_broadcast(shape),
+                in1=for_even[:, span, :, :].unsqueeze(2).to_broadcast(shape),
+                op=MULT,
+            )
+            nc.vector.tensor_tensor(
+                out=from_odd[:].rearrange("p (t h e i) -> p t h e i", t=tiles, h=heads, e=2),
+                in0=y[:, :, :, 1:2, :].to_broadcast(shape),
+                in1=for_odd[:, span, :, :].unsqueeze(2).to_broadcast(shape),
+                op=MULT,
+            )
+            nc.gpsimd.tensor_tensor(
+                out=rotated[:, :, span, :].rearrange("p h t (i e) -> p t h i e", e=2),
+                in0=from_even[:].rearrange("p (t h e i) -> p t h i e", t=tiles, h=heads, e=2),
+                in1=from_odd[:].rearrange("p (t h e i) -> p t h i e", t=tiles, h=heads, e=2),
+                op=ADD,
+            )
+
+        def store(view, result, last_tile):
+            if (last_tile + 1) % STORE_TILES == 0:
+                span = slice(last_tile + 1 - STORE_TILES, last_tile + 1)
+                nc.sync.dma_start(out=view[:, :, span, :], in_=result[:, :, span, :])
+
+        for t in range(X_CHUNK):
+            quantise_x(t)
+        quantise_weights(0, nc.vector.tensor_copy)
+        for t in range(X_CHUNK, TILES):
+            quantise_x(t)
+        for r in range(1, ROUNDS):
+            quantise_weights(r, nc.scalar.copy)
+
+        for r in range(Q_ROUNDS):
+            heads = slice(r * BANK_HEADS, (r + 1) * BANK_HEADS)
+            for t in range(TILES):
+                q_sums = banks.tile([P, BANK], F32, tag="bank")
+                project(q_sums[:], t, r, slice(0, BANK))
+                rotate(q_sums, t, 1, BANK_HEADS, q_rotated[r])
+                store(q_view[:, heads, :, :], q_rotated[r], t)
+
+        for first_tile in range(0, TILES, 2):
+            k_sums = banks.tile([P, BANK], F32, tag="bank")
+            for s in range(2):
+                project(
+                    k_sums[:, s * KV_COLS : (s + 1) * KV_COLS],
+                    first_tile + s,
+                    Q_ROUNDS,
+                    slice(0, KV_COLS),
+                )
+            rotate(k_sums, first_tile, 2, KV_HEADS, k_rotated)
+            store(k_view, k_rotated, first_tile + 1)
+        for first_tile in range(0, TILES, 2):
+            v_sums = banks.tile([P, BANK], F32, tag="bank")
+            for s in range(2):
+                project(
+                    v_sums[:, s * KV_COLS : (s + 1) * KV_COLS],
+                    first_tile + s,
+                    Q_ROUNDS,
+                    slice(KV_COLS, BANK),
+                )
+            nc.scalar.copy(
+                out=v_plain[:, :, first_tile : first_tile + 2, :].rearrange("p h t d -> p t h d"),
+                in_=v_sums[:].rearrange("p (t h d) -> p t h d", t=2, h=KV_HEADS),
+            )
+            store(v_view, v_plain, first_tile + 1)

@@ -75,8 +75,8 @@ def tile_groupedqueryattention_pa_kernel(
         ]
         cos_rows = keep.tile([P, TILES, PAIRS], BF16)
         sin_rows = keep.tile([P, TILES, PAIRS], BF16)
-        for_even = keep.tile([P, TILES, 2, PAIRS], F32)
-        for_odd = keep.tile([P, TILES, 2, PAIRS], F32)
+        for_even = keep.tile([P, TILES, PAIRS, 2], F32)
+        for_odd = keep.tile([P, TILES, PAIRS, 2], F32)
         q_rotated = [
             keep.tile([P, BANK_HEADS, TILES, HEAD], F32, name="q_rotated%d" % r)
             for r in range(Q_ROUNDS)
@@ -109,10 +109,10 @@ def tile_groupedqueryattention_pa_kernel(
 
         make_identity(nc, identity[:])
 
-        nc.scalar.copy(out=for_even[:, :, 0, :], in_=cos_rows[:])
-        nc.scalar.copy(out=for_odd[:, :, 1, :], in_=cos_rows[:])
-        nc.vector.tensor_copy(out=for_even[:, :, 1, :], in_=sin_rows[:])
-        nc.vector.tensor_scalar_mul(out=for_odd[:, :, 0, :], in0=sin_rows[:], scalar1=-1.0)
+        nc.scalar.copy(out=for_even[:, :, :, 0], in_=cos_rows[:])
+        nc.scalar.copy(out=for_odd[:, :, :, 1], in_=cos_rows[:])
+        nc.vector.tensor_copy(out=for_even[:, :, :, 1], in_=sin_rows[:])
+        nc.vector.tensor_scalar_mul(out=for_odd[:, :, :, 0], in0=sin_rows[:], scalar1=-1.0)
 
         def quantise_x(t):
             words = x_rows[:, t, :].bitcast(F32)
@@ -163,27 +163,27 @@ def tile_groupedqueryattention_pa_kernel(
                 )
 
         def rotate(bank, first_tile, tiles, heads, rotated):
-            shape = [P, tiles, heads, 2, PAIRS]
-            y = bank[:].rearrange("p (t h i e) -> p t h e i", t=tiles, h=heads, e=2)
+            shape = [P, tiles, heads, PAIRS, 2]
+            y = bank[:].rearrange("p (t h i e) -> p t h i e", t=tiles, h=heads, e=2)
             span = slice(first_tile, first_tile + tiles)
             from_even = products.tile([P, BANK], F32, tag="from_even")
             from_odd = products.tile([P, BANK], F32, tag="from_odd")
             nc.vector.tensor_tensor(
-                out=from_even[:].rearrange("p (t h e i) -> p t h e i", t=tiles, h=heads, e=2),
-                in0=y[:, :, :, 0:1, :].to_broadcast(shape),
+                out=from_even[:].rearrange("p (t h i e) -> p t h i e", t=tiles, h=heads, e=2),
+                in0=y[:, :, :, :, 0:1].to_broadcast(shape),
                 in1=for_even[:, span, :, :].unsqueeze(2).to_broadcast(shape),
                 op=MULT,
             )
             nc.vector.tensor_tensor(
-                out=from_odd[:].rearrange("p (t h e i) -> p t h e i", t=tiles, h=heads, e=2),
-                in0=y[:, :, :, 1:2, :].to_broadcast(shape),
+                out=from_odd[:].rearrange("p (t h i e) -> p t h i e", t=tiles, h=heads, e=2),
+                in0=y[:, :, :, :, 1:2].to_broadcast(shape),
                 in1=for_odd[:, span, :, :].unsqueeze(2).to_broadcast(shape),
                 op=MULT,
             )
             nc.gpsimd.tensor_tensor(
-                out=rotated[:, :, span, :].rearrange("p h t (i e) -> p t h i e", e=2),
-                in0=from_even[:].rearrange("p (t h e i) -> p t h i e", t=tiles, h=heads, e=2),
-                in1=from_odd[:].rearrange("p (t h e i) -> p t h i e", t=tiles, h=heads, e=2),
+                out=rotated[:, :, span, :].rearrange("p h t d -> p t h d"),
+                in0=from_even[:].rearrange("p (t h d) -> p t h d", t=tiles, h=heads),
+                in1=from_odd[:].rearrange("p (t h d) -> p t h d", t=tiles, h=heads),
                 op=ADD,
             )
 

@@ -22,16 +22,19 @@ HEAD = 128
 PAIRS = HEAD // 2
 BANK = 512
 Q_HEADS = 8
-KV_HEADS = 2
-BANK_HEADS = BANK // HEAD
-Q_ROUNDS = Q_HEADS // BANK_HEADS
-ROUNDS = Q_ROUNDS + 1
-KV_COLS = KV_HEADS * HEAD
+UNIT_HEADS = 2
+UNIT_COLS = UNIT_HEADS * HEAD
+DUO = 2
+DUOS = TILES // DUO
+Q_UNITS = Q_HEADS // UNIT_HEADS
+Q_LOAD_UNITS = 2
 WORDS = K_PASS // 2
-X_CHUNK = 2
-STORE_TILES = 4
+HALF_TILES = BANK // HEAD
+LEAD = 2
+QUANT_AHEAD = 1
+SPLIT_HEADS = (5, 7)
 
-FLOPS = 2 * TOKENS * FEATURES * (Q_HEADS + 2 * KV_HEADS) * HEAD
+FLOPS = 2 * TOKENS * FEATURES * (Q_HEADS + 2 * UNIT_HEADS) * HEAD
 
 
 def tile_groupedqueryattention_pa_kernel(
@@ -40,8 +43,9 @@ def tile_groupedqueryattention_pa_kernel(
     nc = tc.nc
     with ExitStack() as stack:
         keep = stack.enter_context(tc.tile_pool(name="keep", bufs=1))
-        products = stack.enter_context(tc.tile_pool(name="products", bufs=4))
+        products = stack.enter_context(tc.tile_pool(name="products", bufs=3))
         banks = stack.enter_context(tc.psum_pool(name="banks", bufs=8))
+        stack.enter_context(tc.manual_schedule())
 
         x_view = x[0].rearrange("(p t) k -> p t k", t=TILES)
         cos_view = rope_cos[0].rearrange("(p t) i -> p t i", t=TILES)
@@ -54,68 +58,80 @@ def tile_groupedqueryattention_pa_kernel(
         v_view = out_2[0].rearrange("h (p t) d -> p h t d", t=TILES)
 
         identity = keep.tile([P, P], F32)
-        x_rows = keep.tile([P, TILES, FEATURES], BF16)
-        x_grouped = keep.tile([P, TILES, FEATURES], BF16, align_bytes=64)
-        x_codes = keep.tile([P, TILES, PASSES * P], U32, align_bytes=64)
-        x_scales = keep.tile([P, TILES, PASSES * P], U8, align_bytes=64)
-        w_rows = [
-            keep.tile([P, PASSES, PACK, BANK], BF16, name="w_rows%d" % r) for r in range(ROUNDS)
+        x_rows = [keep.tile([P, DUO, FEATURES], BF16, name="x_rows%d" % d) for d in range(DUOS)]
+        x_grouped = [
+            keep.tile([P, DUO, FEATURES], BF16, name="x_grouped%d" % d, align_bytes=64)
+            for d in range(DUOS)
         ]
-        w_grouped = [
-            keep.tile([P, PASSES, BANK, PACK], BF16, name="w_grouped%d" % r, align_bytes=64)
-            for r in range(ROUNDS)
+        x_codes = [
+            keep.tile([P, DUO, PASSES, P], U32, name="x_codes%d" % d, align_bytes=64)
+            for d in range(DUOS)
         ]
-        w_codes = [
-            keep.tile([P, PASSES, BANK], U32, name="w_codes%d" % r, align_bytes=64)
-            for r in range(ROUNDS)
+        x_scales = [
+            keep.tile([P, DUO, PASSES, P], U8, name="x_scales%d" % d, align_bytes=64)
+            for d in range(DUOS)
         ]
-        w_scales = [
-            keep.tile([P, PASSES, BANK], U8, name="w_scales%d" % r, align_bytes=64)
-            for r in range(ROUNDS)
+        k_rows = [keep.tile([P, PACK, UNIT_COLS], BF16, name="k_rows%d" % g) for g in range(PASSES)]
+        v_rows = [keep.tile([P, PACK, UNIT_COLS], BF16, name="v_rows%d" % g) for g in range(PASSES)]
+        q_rows = [
+            [
+                keep.tile([P, PACK, Q_LOAD_UNITS * UNIT_COLS], BF16, name="q_rows%d_%d" % (part, g))
+                for g in range(PASSES)
+            ]
+            for part in range(Q_UNITS // Q_LOAD_UNITS)
         ]
-        cos_rows = keep.tile([P, TILES, PAIRS], BF16)
-        sin_rows = keep.tile([P, TILES, PAIRS], BF16)
-        for_even = keep.tile([P, TILES, PAIRS, 2], F32)
-        for_odd = keep.tile([P, TILES, PAIRS, 2], F32)
-        q_rotated = [
-            keep.tile([P, BANK_HEADS, TILES, HEAD], F32, name="q_rotated%d" % r)
-            for r in range(Q_ROUNDS)
-        ]
-        k_rotated = keep.tile([P, KV_HEADS, TILES, HEAD], F32)
-        v_plain = keep.tile([P, KV_HEADS, TILES, HEAD], F32)
 
-        nc.scalar.dma_start(out=cos_rows[:], in_=cos_view)
-        nc.scalar.dma_start(out=sin_rows[:], in_=sin_view)
+        def weight_unit(name, rows_of_pass):
+            return {
+                "rows": rows_of_pass,
+                "grouped": keep.tile(
+                    [P, PASSES, UNIT_COLS, PACK], BF16, name="grouped_" + name, align_bytes=64
+                ),
+                "codes": keep.tile([P, PASSES, UNIT_COLS], U32, name="codes_" + name, align_bytes=64),
+                "scales": keep.tile([P, PASSES, UNIT_COLS], U8, name="scales_" + name, align_bytes=64),
+            }
 
-        def load_x(chunk):
-            tiles = slice(chunk * X_CHUNK, (chunk + 1) * X_CHUNK)
-            nc.sync.dma_start(out=x_rows[:, tiles, :], in_=x_view[:, tiles, :])
+        k_unit = weight_unit("k", [rows[:] for rows in k_rows])
+        v_unit = weight_unit("v", [rows[:] for rows in v_rows])
+        q_units = []
+        for u in range(Q_UNITS):
+            part, place = divmod(u, Q_LOAD_UNITS)
+            cols = slice(place * UNIT_COLS, (place + 1) * UNIT_COLS)
+            q_units.append(weight_unit("q%d" % u, [q_rows[part][g][:, :, cols] for g in range(PASSES)]))
 
-        def load_weights(r):
-            for g in range(PASSES):
-                if r < Q_ROUNDS:
-                    cols = slice(r * BANK, (r + 1) * BANK)
-                    nc.sync.dma_start(out=w_rows[r][:, g, :, :], in_=wq_view[g, :, :, cols])
-                else:
-                    nc.sync.dma_start(out=w_rows[r][:, g, :, 0:KV_COLS], in_=wk_view[g])
-                    nc.sync.dma_start(out=w_rows[r][:, g, :, KV_COLS:BANK], in_=wv_view[g])
+        factors = keep.tile([P, 2, 2, TILES, PAIRS], BF16)
+        k_result = keep.tile([P, UNIT_HEADS, TILES, HEAD], F32)
+        v_result = keep.tile([P, UNIT_HEADS, TILES, HEAD], F32)
+        q_result = [keep.tile([P, TILES, HEAD], F32, name="q_result%d" % h) for h in range(Q_HEADS)]
+
+        def load_x(d):
+            nc.sync.dma_start(out=x_rows[d][:], in_=x_view[:, d * DUO : (d + 1) * DUO, :])
 
         load_x(0)
-        load_weights(0)
-        for chunk in range(1, TILES // X_CHUNK):
-            load_x(chunk)
-        for r in range(1, ROUNDS):
-            load_weights(r)
+        for g in range(PASSES):
+            nc.sync.dma_start(out=k_rows[g][:], in_=wk_view[g])
+        load_x(1)
+        nc.sync.dma_start(out=factors[:, 0, 1, :, :], in_=sin_view)
+        nc.sync.dma_start(out=factors[:, 0, 0, :, :], in_=cos_view)
+        nc.sync.dma_start(out=factors[:, 1, 1, :, :], in_=cos_view)
+        for d in range(2, DUOS):
+            load_x(d)
+        for part in range(Q_UNITS // Q_LOAD_UNITS):
+            cols = slice(part * Q_LOAD_UNITS * UNIT_COLS, (part + 1) * Q_LOAD_UNITS * UNIT_COLS)
+            for g in range(PASSES):
+                nc.sync.dma_start(out=q_rows[part][g][:], in_=wq_view[g, :, :, cols])
+        for g in range(PASSES):
+            nc.sync.dma_start(out=v_rows[g][:], in_=wv_view[g])
 
         make_identity(nc, identity[:])
+        nc.gpsimd.tensor_scalar(
+            out=factors[:, 1, 0, :, :], in0=factors[:, 0, 1, :, :],
+            scalar1=-1.0, scalar2=0.0, op0=MULT, op1=ADD,
+        )
 
-        nc.scalar.copy(out=for_even[:, :, :, 0], in_=cos_rows[:])
-        nc.scalar.copy(out=for_odd[:, :, :, 1], in_=cos_rows[:])
-        nc.vector.tensor_copy(out=for_even[:, :, :, 1], in_=sin_rows[:])
-        nc.vector.tensor_scalar_mul(out=for_odd[:, :, :, 0], in0=sin_rows[:], scalar1=-1.0)
-
-        def quantise_x(t):
-            words = x_rows[:, t, :].bitcast(F32)
+        def turn_x(t):
+            d, s = divmod(t, DUO)
+            words = x_rows[d][:, s, :].bitcast(F32)
             turned = banks.tile([P, BANK], F32, tag="bank")
             for g in range(PASSES):
                 for u in range(2):
@@ -127,109 +143,183 @@ def tile_groupedqueryattention_pa_kernel(
                         identity[:],
                     )
             nc.scalar.copy(
-                out=x_grouped[:, t, :].bitcast(F32).rearrange("p (g n u) -> p g n u", g=PASSES, u=2),
+                out=x_grouped[d][:, s, :]
+                .bitcast(F32)
+                .rearrange("p (g n u) -> p g n u", g=PASSES, u=2),
                 in_=turned[:].rearrange("p (g u n) -> p g n u", g=PASSES, u=2),
             )
+
+        def quantise_x(d):
             nc.vector.quantize_mx(
-                out=x_codes[:, t, :].bitcast(FP8X4),
-                scales=x_scales[:, t, :],
-                in_=x_grouped[:, t, :],
+                out=x_codes[d][:].rearrange("p s g n -> p (s g n)").bitcast(FP8X4),
+                scales=x_scales[d][:].rearrange("p s g n -> p (s g n)"),
+                in_=x_grouped[d][:].rearrange("p s k -> p (s k)"),
             )
 
-        def quantise_weights(r, copy):
+        def group_weights(unit, copy):
             for g in range(PASSES):
                 copy(
-                    out=w_grouped[r][:, g, :, :].rearrange("p (c i) j -> p c j i", i=4),
-                    in_=w_rows[r][:, g, :, :].rearrange("p j (c i) -> p c j i", i=4),
-                )
-            for g in range(PASSES):
-                nc.vector.quantize_mx(
-                    out=w_codes[r][:, g, :].bitcast(FP8X4),
-                    scales=w_scales[r][:, g, :],
-                    in_=w_grouped[r][:, g, :, :].rearrange("p c j -> p (c j)"),
+                    out=unit["grouped"][:, g, :, :].rearrange("p (c i) j -> p c j i", i=4),
+                    in_=unit["rows"][g].rearrange("p j (c i) -> p c j i", i=4),
                 )
 
-        def project(sums, t, r, cols):
-            for g in range(PASSES):
-                tokens = slice(g * P, (g + 1) * P)
-                nc.tensor.matmul_mx(
-                    out=sums,
-                    lhsT=x_codes[:, t, tokens].bitcast(FP8X4),
-                    lhsT_scale=x_scales[:, t, tokens],
-                    rhs=w_codes[r][:, g, cols].bitcast(FP8X4),
-                    rhs_scale=w_scales[r][:, g, cols],
-                    start=(g == 0),
-                    stop=(g == PASSES - 1),
-                )
+        def quantise_weights(unit):
+            nc.vector.quantize_mx(
+                out=unit["codes"][:].rearrange("p g c -> p (g c)").bitcast(FP8X4),
+                scales=unit["scales"][:].rearrange("p g c -> p (g c)"),
+                in_=unit["grouped"][:].rearrange("p g c j -> p (g c j)"),
+            )
 
-        def rotate(bank, first_tile, tiles, heads, rotated):
-            shape = [P, tiles, heads, PAIRS, 2]
-            y = bank[:].rearrange("p (t h i e) -> p t h i e", t=tiles, h=heads, e=2)
-            span = slice(first_tile, first_tile + tiles)
-            from_even = products.tile([P, BANK], F32, tag="from_even")
-            from_odd = products.tile([P, BANK], F32, tag="from_odd")
+        def project(unit, heads, tiles):
+            sums = banks.tile([P, BANK], F32, tag="bank")
+            place = 0
+            for h in heads:
+                for t in tiles:
+                    d, s = divmod(t, DUO)
+                    for g in range(PASSES):
+                        nc.tensor.matmul_mx(
+                            out=sums[:, place * HEAD : (place + 1) * HEAD],
+                            lhsT=x_codes[d][:, s, g, :].bitcast(FP8X4),
+                            lhsT_scale=x_scales[d][:, s, g, :],
+                            rhs=unit["codes"][:, g, h * HEAD : (h + 1) * HEAD].bitcast(FP8X4),
+                            rhs_scale=unit["scales"][:, g, h * HEAD : (h + 1) * HEAD],
+                            start=(g == 0),
+                            stop=(g == PASSES - 1),
+                        )
+                    place += 1
+            return sums
+
+        def multiply(sums, place, tiles, both):
+            width = len(tiles) * HEAD
+            shape = [P, 2, width // 2, 2]
+            y = sums[:, place * HEAD : place * HEAD + width].rearrange("p (m a) -> p a m", a=2)
             nc.vector.tensor_tensor(
-                out=from_even[:].rearrange("p (t h i e) -> p t h i e", t=tiles, h=heads, e=2),
-                in0=y[:, :, :, :, 0:1].to_broadcast(shape),
-                in1=for_even[:, span, :, :].unsqueeze(2).to_broadcast(shape),
+                out=both.rearrange("p a (m e) -> p a m e", e=2),
+                in0=y.unsqueeze(3).to_broadcast(shape),
+                in1=factors[:, :, :, tiles[0] : tiles[0] + len(tiles), :].rearrange(
+                    "p a e t i -> p a (t i) e"
+                ),
                 op=MULT,
             )
-            nc.vector.tensor_tensor(
-                out=from_odd[:].rearrange("p (t h i e) -> p t h i e", t=tiles, h=heads, e=2),
-                in0=y[:, :, :, :, 1:2].to_broadcast(shape),
-                in1=for_odd[:, span, :, :].unsqueeze(2).to_broadcast(shape),
-                op=MULT,
+
+        jobs = []
+        for d in range(DUOS):
+            tiles = list(range(d * DUO, (d + 1) * DUO))
+            jobs.append(
+                {
+                    "unit": k_unit,
+                    "banks": [(list(range(UNIT_HEADS)), tiles)],
+                    "adder": nc.gpsimd,
+                    "out": k_result[:, :, tiles[0] : tiles[0] + DUO, :].rearrange("p h t f -> p h (t f)"),
+                    "stores": [
+                        (k_view[:, :, tiles[0] - DUO : tiles[0] + DUO, :],
+                         k_result[:, :, tiles[0] - DUO : tiles[0] + DUO, :])
+                    ] if d % 2 == 1 else [],
+                }
             )
-            nc.gpsimd.tensor_tensor(
-                out=rotated[:, :, span, :].rearrange("p h t d -> p t h d"),
-                in0=from_even[:].rearrange("p (t h d) -> p t h d", t=tiles, h=heads),
-                in1=from_odd[:].rearrange("p (t h d) -> p t h d", t=tiles, h=heads),
-                op=ADD,
-            )
-
-        def store(view, result, last_tile):
-            if (last_tile + 1) % STORE_TILES == 0:
-                span = slice(last_tile + 1 - STORE_TILES, last_tile + 1)
-                nc.sync.dma_start(out=view[:, :, span, :], in_=result[:, :, span, :])
-
-        for t in range(X_CHUNK):
-            quantise_x(t)
-        quantise_weights(0, nc.vector.tensor_copy)
-        for t in range(X_CHUNK, TILES):
-            quantise_x(t)
-        for r in range(1, ROUNDS):
-            quantise_weights(r, nc.scalar.copy)
-
-        for r in range(Q_ROUNDS):
-            heads = slice(r * BANK_HEADS, (r + 1) * BANK_HEADS)
-            for t in range(TILES):
-                q_sums = banks.tile([P, BANK], F32, tag="bank")
-                project(q_sums[:], t, r, slice(0, BANK))
-                rotate(q_sums, t, 1, BANK_HEADS, q_rotated[r])
-                store(q_view[:, heads, :, :], q_rotated[r], t)
-
-        for first_tile in range(0, TILES, 2):
-            k_sums = banks.tile([P, BANK], F32, tag="bank")
-            for s in range(2):
-                project(
-                    k_sums[:, s * KV_COLS : (s + 1) * KV_COLS],
-                    first_tile + s,
-                    Q_ROUNDS,
-                    slice(0, KV_COLS),
+        for h in range(Q_HEADS):
+            halves = [list(range(first, first + HALF_TILES)) for first in range(0, TILES, HALF_TILES)]
+            if h in SPLIT_HEADS:
+                for b, tiles in enumerate(halves):
+                    span = slice(tiles[0], tiles[0] + HALF_TILES)
+                    jobs.append(
+                        {
+                            "unit": q_units[h // UNIT_HEADS],
+                            "banks": [([h % UNIT_HEADS], tiles)],
+                            "adder": nc.vector if b == 1 else nc.gpsimd,
+                            "out": q_result[h][:, span, :].rearrange("p (b t) f -> p b (t f)", b=1),
+                            "stores": [(q_view[:, h, span, :], q_result[h][:, span, :])],
+                        }
+                    )
+            else:
+                jobs.append(
+                    {
+                        "unit": q_units[h // UNIT_HEADS],
+                        "banks": [([h % UNIT_HEADS], tiles) for tiles in halves],
+                        "adder": nc.gpsimd,
+                        "out": q_result[h][:].rearrange("p (b t) f -> p b (t f)", b=len(halves)),
+                        "stores": [(q_view[:, h, :, :], q_result[h][:])],
+                    }
                 )
-            rotate(k_sums, first_tile, 2, KV_HEADS, k_rotated)
-            store(k_view, k_rotated, first_tile + 1)
-        for first_tile in range(0, TILES, 2):
-            v_sums = banks.tile([P, BANK], F32, tag="bank")
-            for s in range(2):
-                project(
-                    v_sums[:, s * KV_COLS : (s + 1) * KV_COLS],
-                    first_tile + s,
-                    Q_ROUNDS,
-                    slice(KV_COLS, BANK),
+        flat = [(j, b) for j, job in enumerate(jobs) for b in range(len(job["banks"]))]
+        sums_of = {}
+        both_of = {}
+
+        def start_bank(n):
+            j, b = flat[n]
+            heads, tiles = jobs[j]["banks"][b]
+            sums_of[n] = project(jobs[j]["unit"], heads, tiles)
+
+        def rotate_bank(n, between=None):
+            j, b = flat[n]
+            job = jobs[j]
+            heads, tiles = job["banks"][b]
+            width = len(tiles) * HEAD
+            if b == 0:
+                both_of[j] = products.tile([P, 2 * BANK // width, 2, width], F32, tag="both", name="both%d" % j)
+            for place, h in enumerate(heads):
+                multiply(sums_of[n], place * len(tiles), tiles, both_of[j][:, b * len(heads) + place, :, :])
+                if place == 0 and between is not None:
+                    between()
+            if b == len(job["banks"]) - 1:
+                used = len(job["banks"]) * len(heads)
+                job["adder"].tensor_tensor(
+                    out=job["out"],
+                    in0=both_of[j][:, 0:used, 0, :],
+                    in1=both_of[j][:, 0:used, 1, :],
+                    op=ADD,
                 )
+                for view, result in job["stores"]:
+                    nc.sync.dma_start(out=view, in_=result)
+
+        def values(d):
+            tiles = list(range(d * DUO, (d + 1) * DUO))
+            sums = project(v_unit, list(range(UNIT_HEADS)), tiles)
             nc.scalar.copy(
-                out=v_plain[:, :, first_tile : first_tile + 2, :].rearrange("p h t d -> p t h d"),
-                in_=v_sums[:].rearrange("p (t h d) -> p t h d", t=2, h=KV_HEADS),
+                out=v_result[:, :, tiles[0] : tiles[0] + DUO, :].rearrange("p h t f -> p h (t f)"),
+                in_=sums[:].rearrange("p (h m) -> p h m", h=UNIT_HEADS),
             )
-            store(v_view, v_plain, first_tile + 1)
+            if d % 2 == 1:
+                span = slice(tiles[0] - DUO, tiles[0] + DUO)
+                nc.sync.dma_start(out=v_view[:, :, span, :], in_=v_result[:, :, span, :])
+
+        turn_x(0)
+        turn_x(1)
+        group_weights(k_unit, nc.vector.tensor_copy)
+        quantise_weights(k_unit)
+        quantise_x(0)
+        turn_x(2)
+        turn_x(3)
+        start_bank(0)
+        turn_x(4)
+        turn_x(5)
+
+        def next_duo(d):
+            quantise_x(d)
+            start_bank(d)
+
+        rotate_bank(0, lambda: next_duo(1))
+        turn_x(6)
+        turn_x(7)
+        for unit in q_units + [v_unit]:
+            group_weights(unit, nc.scalar.copy)
+        rotate_bank(1, lambda: next_duo(2))
+        rotate_bank(2, lambda: next_duo(3))
+        rotate_bank(3, lambda: quantise_weights(q_units[0]))
+
+        started = DUOS
+        first_value_step = len(flat) - 2 * DUOS
+        quantised_units = 1
+        for n in range(DUOS, len(flat)):
+            while started <= min(n + LEAD, len(flat) - 1):
+                start_bank(started)
+                started += 1
+            rotate_bank(n)
+            ahead = min(n + LEAD + QUANT_AHEAD, len(flat) - 1)
+            if quantised_units < Q_UNITS and jobs[flat[ahead][0]]["unit"] is q_units[quantised_units]:
+                quantise_weights(q_units[quantised_units])
+                quantised_units += 1
+            if n == first_value_step - 1:
+                quantise_weights(v_unit)
+            if first_value_step <= n < first_value_step + DUOS:
+                values(n - first_value_step)

@@ -32,7 +32,8 @@ WORDS = K_PASS // 2
 HALF_TILES = BANK // HEAD
 LEAD = 2
 QUANT_AHEAD = 1
-SPLIT_HEADS = (5, 7)
+SPLIT_HEADS = (0, 1, 2, 3, 4, 5, 6, 7)
+VECTOR_ADDS = ((5, 1), (7, 1))
 
 FLOPS = 2 * TOKENS * FEATURES * (Q_HEADS + 2 * UNIT_HEADS) * HEAD
 
@@ -226,7 +227,7 @@ def tile_groupedqueryattention_pa_kernel(
                         {
                             "unit": q_units[h // UNIT_HEADS],
                             "banks": [([h % UNIT_HEADS], tiles)],
-                            "adder": nc.vector if b == 1 else nc.gpsimd,
+                            "adder": nc.vector if (h, b) in VECTOR_ADDS else nc.gpsimd,
                             "out": q_result[h][:, span, :].rearrange("p (b t) f -> p b (t f)", b=1),
                             "stores": [(q_view[:, h, span, :], q_result[h][:, span, :])],
                         }

@@ -33,7 +33,7 @@ HALF_TILES = BANK // HEAD
 LEAD = 2
 QUANT_AHEAD = 1
 SPLIT_HEADS = (0, 1, 2, 3, 4, 5, 6, 7)
-VECTOR_ADDS = ((5, 1), (7, 1))
+VECTOR_ADDS = ((6, 1), (7, 1))
 
 FLOPS = 2 * TOKENS * FEATURES * (Q_HEADS + 2 * UNIT_HEADS) * HEAD
 
@@ -108,11 +108,11 @@ def tile_groupedqueryattention_pa_kernel(
         def load_x(d):
             nc.sync.dma_start(out=x_rows[d][:], in_=x_view[:, d * DUO : (d + 1) * DUO, :])
 
+        nc.sync.dma_start(out=factors[:, 0, 1, :, :], in_=sin_view)
         load_x(0)
         for g in range(PASSES):
             nc.sync.dma_start(out=k_rows[g][:], in_=wk_view[g])
         load_x(1)
-        nc.sync.dma_start(out=factors[:, 0, 1, :, :], in_=sin_view)
         nc.sync.dma_start(out=factors[:, 0, 0, :, :], in_=cos_view)
         nc.sync.dma_start(out=factors[:, 1, 1, :, :], in_=cos_view)
         for d in range(2, DUOS):
@@ -294,19 +294,21 @@ def tile_groupedqueryattention_pa_kernel(
         start_bank(0)
         turn_x(4)
         turn_x(5)
-
-        def next_duo(d):
-            quantise_x(d)
-            start_bank(d)
-
-        rotate_bank(0, lambda: next_duo(1))
+        quantise_x(1)
+        start_bank(1)
+        rotate_bank(0)
         turn_x(6)
         turn_x(7)
         for unit in q_units + [v_unit]:
             group_weights(unit, nc.scalar.copy)
-        rotate_bank(1, lambda: next_duo(2))
-        rotate_bank(2, lambda: next_duo(3))
-        rotate_bank(3, lambda: quantise_weights(q_units[0]))
+        quantise_x(2)
+        start_bank(2)
+        rotate_bank(1)
+        quantise_x(3)
+        start_bank(3)
+        rotate_bank(2)
+        quantise_weights(q_units[0])
+        rotate_bank(3)
 
         started = DUOS
         first_value_step = len(flat) - 2 * DUOS

@@ -33,7 +33,10 @@ HALF_TILES = BANK // HEAD
 LEAD = 2
 QUANT_AHEAD = 1
 SPLIT_HEADS = (0, 1, 2, 3, 4, 5, 6, 7)
-VECTOR_ADDS = ((6, 1), (7, 1))
+TURN_STEP = 12
+GPSIMD_MULTIPLIES = ()
+TURNED = ((6, 0), (6, 1))
+VECTOR_ADDS = ((7, 1),)
 
 FLOPS = 2 * TOKENS * FEATURES * (Q_HEADS + 2 * UNIT_HEADS) * HEAD
 
@@ -61,15 +64,15 @@ def tile_groupedqueryattention_pa_kernel(
         identity = keep.tile([P, P], F32)
         x_rows = [keep.tile([P, DUO, FEATURES], BF16, name="x_rows%d" % d) for d in range(DUOS)]
         x_grouped = [
-            keep.tile([P, DUO, FEATURES], BF16, name="x_grouped%d" % d, align_bytes=64)
+            keep.tile([P, PASSES, DUO, K_PASS], BF16, name="x_grouped%d" % d, align_bytes=64)
             for d in range(DUOS)
         ]
         x_codes = [
-            keep.tile([P, DUO, PASSES, P], U32, name="x_codes%d" % d, align_bytes=64)
+            keep.tile([P, PASSES, DUO, P], U32, name="x_codes%d" % d, align_bytes=64)
             for d in range(DUOS)
         ]
         x_scales = [
-            keep.tile([P, DUO, PASSES, P], U8, name="x_scales%d" % d, align_bytes=64)
+            keep.tile([P, PASSES, DUO, P], U8, name="x_scales%d" % d, align_bytes=64)
             for d in range(DUOS)
         ]
         k_rows = [keep.tile([P, PACK, UNIT_COLS], BF16, name="k_rows%d" % g) for g in range(PASSES)]
@@ -101,6 +104,10 @@ def tile_groupedqueryattention_pa_kernel(
             q_units.append(weight_unit("q%d" % u, [q_rows[part][g][:, :, cols] for g in range(PASSES)]))
 
         factors = keep.tile([P, 2, 2, TILES, PAIRS], BF16)
+        identity_bf16 = keep.tile([P, P], BF16)
+        swap = keep.tile([P, P], F32)
+        spread = keep.tile([P, 2, TILES, HEAD], BF16)
+        turned_factors = keep.tile([P, 2, TILES, P], BF16)
         k_result = keep.tile([P, UNIT_HEADS, TILES, HEAD], F32)
         v_result = keep.tile([P, UNIT_HEADS, TILES, HEAD], F32)
         q_result = [keep.tile([P, TILES, HEAD], F32, name="q_result%d" % h) for h in range(Q_HEADS)]
@@ -125,10 +132,79 @@ def tile_groupedqueryattention_pa_kernel(
             nc.sync.dma_start(out=v_rows[g][:], in_=wv_view[g])
 
         make_identity(nc, identity[:])
+        make_identity(nc, identity_bf16[:])
         nc.gpsimd.tensor_scalar(
             out=factors[:, 1, 0, :, :], in0=factors[:, 0, 1, :, :],
             scalar1=-1.0, scalar2=0.0, op0=MULT, op1=ADD,
         )
+
+        pairs_of_identity = identity[:].rearrange("p (i e) -> p i e", e=2)
+        pairs_of_swap = swap[:].rearrange("p (i e) -> p i e", e=2)
+        for e in range(2):
+            nc.gpsimd.tensor_copy(out=pairs_of_swap[:, :, e], in_=pairs_of_identity[:, :, 1 - e])
+
+        def spread_factors():
+            flat_factors = factors[:].rearrange("p a e t i -> p (a e) (t i)")
+            nc.scalar.copy(
+                out=spread[:, 0, :, :].rearrange("p t (i e) -> p (t i) e", e=2),
+                in_=flat_factors[:, 0:4:3, :].rearrange("p z m -> p m z"),
+            )
+            nc.scalar.copy(
+                out=spread[:, 1, :, :].rearrange("p t (i e) -> p (t i) e", e=2),
+                in_=flat_factors[:, 1:3, :].rearrange("p z m -> p m z"),
+            )
+
+        def turn_factors():
+            for a in range(2):
+                turned = banks.tile([P, TILES * P], BF16, tag="bank")
+                for t in range(TILES):
+                    nc.tensor.transpose(turned[:, t * P : (t + 1) * P], spread[:, a, t, :], identity_bf16[:])
+                nc.scalar.copy(out=turned_factors[:, a, :, :].rearrange("p t n -> p (t n)"), in_=turned[:])
+
+        def project_turned(unit, h, tiles):
+            sums = banks.tile([P, BANK], F32, tag="bank")
+            for place, d in enumerate(range(tiles[0] // DUO, tiles[0] // DUO + len(tiles) // DUO)):
+                for g in range(PASSES):
+                    nc.tensor.matmul_mx(
+                        out=sums[:, place * DUO * P : (place + 1) * DUO * P],
+                        lhsT=unit["codes"][:, g, h * HEAD : (h + 1) * HEAD].bitcast(FP8X4),
+                        lhsT_scale=unit["scales"][:, g, h * HEAD : (h + 1) * HEAD],
+                        rhs=x_codes[d][:, g, :, :].rearrange("p s n -> p (s n)").bitcast(FP8X4),
+                        rhs_scale=x_scales[d][:, g, :, :].rearrange("p s n -> p (s n)"),
+                        start=(g == 0),
+                        stop=(g == PASSES - 1),
+                    )
+            return sums
+
+        def rotate_turned(sums, tiles, result, on_gpsimd):
+            both = products.tile([P, 2, BANK], F32, tag="both")
+            engine = nc.vector
+            if on_gpsimd:
+                copied = products.tile([P, BANK], F32, tag="copied")
+                nc.scalar.copy(out=copied[:], in_=sums[:])
+                sums = copied
+                engine = nc.gpsimd
+            engine.tensor_tensor(
+                out=both[:],
+                in0=sums[:].unsqueeze(1).to_broadcast([P, 2, BANK]),
+                in1=turned_factors[:, :, tiles[0] : tiles[0] + len(tiles), :].rearrange("p a t n -> p a (t n)"),
+                op=MULT,
+            )
+            return both
+
+        def turn_back(both, tiles, result):
+            rotated = banks.tile([P, BANK], F32, tag="bank")
+            for place in range(len(tiles)):
+                cols = slice(place * P, (place + 1) * P)
+                nc.tensor.matmul(
+                    out=rotated[:, cols], lhsT=both[:, 0, cols], rhs=identity[:],
+                    is_transpose=True, start=True, stop=False,
+                )
+                nc.tensor.matmul(
+                    out=rotated[:, cols], lhsT=both[:, 1, cols], rhs=swap[:],
+                    is_transpose=True, start=False, stop=True,
+                )
+            nc.scalar.copy(out=result, in_=rotated[:])
 
         def turn_x(t):
             d, s = divmod(t, DUO)
@@ -144,17 +220,15 @@ def tile_groupedqueryattention_pa_kernel(
                         identity[:],
                     )
             nc.scalar.copy(
-                out=x_grouped[d][:, s, :]
-                .bitcast(F32)
-                .rearrange("p (g n u) -> p g n u", g=PASSES, u=2),
+                out=x_grouped[d][:, :, s, :].bitcast(F32).rearrange("p g (n u) -> p g n u", u=2),
                 in_=turned[:].rearrange("p (g u n) -> p g n u", g=PASSES, u=2),
             )
 
         def quantise_x(d):
             nc.vector.quantize_mx(
-                out=x_codes[d][:].rearrange("p s g n -> p (s g n)").bitcast(FP8X4),
-                scales=x_scales[d][:].rearrange("p s g n -> p (s g n)"),
-                in_=x_grouped[d][:].rearrange("p s k -> p (s k)"),
+                out=x_codes[d][:].rearrange("p g s n -> p (g s n)").bitcast(FP8X4),
+                scales=x_scales[d][:].rearrange("p g s n -> p (g s n)"),
+                in_=x_grouped[d][:].rearrange("p g s k -> p (g s k)"),
             )
 
         def group_weights(unit, copy):
@@ -180,8 +254,8 @@ def tile_groupedqueryattention_pa_kernel(
                     for g in range(PASSES):
                         nc.tensor.matmul_mx(
                             out=sums[:, place * HEAD : (place + 1) * HEAD],
-                            lhsT=x_codes[d][:, s, g, :].bitcast(FP8X4),
-                            lhsT_scale=x_scales[d][:, s, g, :],
+                            lhsT=x_codes[d][:, g, s, :].bitcast(FP8X4),
+                            lhsT_scale=x_scales[d][:, g, s, :],
                             rhs=unit["codes"][:, g, h * HEAD : (h + 1) * HEAD].bitcast(FP8X4),
                             rhs_scale=unit["scales"][:, g, h * HEAD : (h + 1) * HEAD],
                             start=(g == 0),
@@ -228,6 +302,8 @@ def tile_groupedqueryattention_pa_kernel(
                             "unit": q_units[h // UNIT_HEADS],
                             "banks": [([h % UNIT_HEADS], tiles)],
                             "adder": nc.vector if (h, b) in VECTOR_ADDS else nc.gpsimd,
+                            "turned": (h, b) in TURNED,
+                            "on_gpsimd": (h, b) in GPSIMD_MULTIPLIES,
                             "out": q_result[h][:, span, :].rearrange("p (b t) f -> p b (t f)", b=1),
                             "stores": [(q_view[:, h, span, :], q_result[h][:, span, :])],
                         }
@@ -245,17 +321,25 @@ def tile_groupedqueryattention_pa_kernel(
         flat = [(j, b) for j, job in enumerate(jobs) for b in range(len(job["banks"]))]
         sums_of = {}
         both_of = {}
+        unfinished = []
 
         def start_bank(n):
             j, b = flat[n]
             heads, tiles = jobs[j]["banks"][b]
-            sums_of[n] = project(jobs[j]["unit"], heads, tiles)
+            if jobs[j].get("turned", False):
+                sums_of[n] = project_turned(jobs[j]["unit"], heads[0], tiles)
+            else:
+                sums_of[n] = project(jobs[j]["unit"], heads, tiles)
 
         def rotate_bank(n, between=None):
             j, b = flat[n]
             job = jobs[j]
             heads, tiles = job["banks"][b]
             width = len(tiles) * HEAD
+            if job.get("turned", False):
+                both = rotate_turned(sums_of[n], tiles, job["out"][:, 0, :], job["on_gpsimd"])
+                unfinished.append((both, tiles, job))
+                return
             if b == 0:
                 both_of[j] = products.tile([P, 2 * BANK // width, 2, width], F32, tag="both", name="both%d" % j)
             for place, h in enumerate(heads):
@@ -272,6 +356,13 @@ def tile_groupedqueryattention_pa_kernel(
                 )
                 for view, result in job["stores"]:
                     nc.sync.dma_start(out=view, in_=result)
+
+        def finish_turned():
+            for both, tiles, job in unfinished:
+                turn_back(both, tiles, job["out"][:, 0, :])
+                for view, result in job["stores"]:
+                    nc.sync.dma_start(out=view, in_=result)
+            unfinished.clear()
 
         def values(d):
             tiles = list(range(d * DUO, (d + 1) * DUO))
@@ -317,6 +408,7 @@ def tile_groupedqueryattention_pa_kernel(
             while started <= min(n + LEAD, len(flat) - 1):
                 start_bank(started)
                 started += 1
+            finish_turned()
             rotate_bank(n)
             ahead = min(n + LEAD + QUANT_AHEAD, len(flat) - 1)
             if quantised_units < Q_UNITS and jobs[flat[ahead][0]]["unit"] is q_units[quantised_units]:
@@ -324,5 +416,9 @@ def tile_groupedqueryattention_pa_kernel(
                 quantised_units += 1
             if n == first_value_step - 1:
                 quantise_weights(v_unit)
+            if n == TURN_STEP:
+                spread_factors()
+                turn_factors()
             if first_value_step <= n < first_value_step + DUOS:
                 values(n - first_value_step)
+        finish_turned()

@@ -30,12 +30,14 @@ Q_UNITS = Q_HEADS // UNIT_HEADS
 Q_LOAD_UNITS = 2
 WORDS = K_PASS // 2
 HALF_TILES = BANK // HEAD
+GROUP_STEPS = (6, 7, 8, 9, 10, 11)
 LEAD = 2
 QUANT_AHEAD = 1
-SPLIT_HEADS = (0, 1, 2, 3, 4, 5, 6, 7)
-TURN_STEP = 12
-GPSIMD_MULTIPLIES = ()
-TURNED = ((6, 0), (6, 1))
+TURNED = ((2,0),(4,0),(6,0))
+ON_GPSIMD = ()
+TURN_DELAY = 1
+BACK_FIRST = True
+GPSIMD_DELAY = 3
 VECTOR_ADDS = ((7, 1),)
 
 FLOPS = 2 * TOKENS * FEATURES * (Q_HEADS + 2 * UNIT_HEADS) * HEAD
@@ -47,7 +49,7 @@ def tile_groupedqueryattention_pa_kernel(
     nc = tc.nc
     with ExitStack() as stack:
         keep = stack.enter_context(tc.tile_pool(name="keep", bufs=1))
-        products = stack.enter_context(tc.tile_pool(name="products", bufs=3))
+        products = stack.enter_context(tc.tile_pool(name="products", bufs=5))
         banks = stack.enter_context(tc.psum_pool(name="banks", bufs=8))
         stack.enter_context(tc.manual_schedule())
 
@@ -62,7 +64,7 @@ def tile_groupedqueryattention_pa_kernel(
         v_view = out_2[0].rearrange("h (p t) d -> p h t d", t=TILES)
 
         identity = keep.tile([P, P], F32)
-        x_rows = [keep.tile([P, DUO, FEATURES], BF16, name="x_rows%d" % d) for d in range(DUOS)]
+        x_rows = [keep.tile([P, FEATURES], BF16, name="x_rows%d" % t) for t in range(TILES)]
         x_grouped = [
             keep.tile([P, PASSES, DUO, K_PASS], BF16, name="x_grouped%d" % d, align_bytes=64)
             for d in range(DUOS)
@@ -106,20 +108,22 @@ def tile_groupedqueryattention_pa_kernel(
         factors = keep.tile([P, 2, 2, TILES, PAIRS], BF16)
         identity_bf16 = keep.tile([P, P], BF16)
         swap = keep.tile([P, P], F32)
-        spread = keep.tile([P, 2, TILES, HEAD], BF16)
+        spreaders = keep.tile([P, 2, 2, HEAD], BF16)
+        pair_rows = keep.tile([P, 2, TILES // 2, P], BF16)
         turned_factors = keep.tile([P, 2, TILES, P], BF16)
         k_result = keep.tile([P, UNIT_HEADS, TILES, HEAD], F32)
         v_result = keep.tile([P, UNIT_HEADS, TILES, HEAD], F32)
         q_result = [keep.tile([P, TILES, HEAD], F32, name="q_result%d" % h) for h in range(Q_HEADS)]
 
         def load_x(d):
-            nc.sync.dma_start(out=x_rows[d][:], in_=x_view[:, d * DUO : (d + 1) * DUO, :])
+            for t in range(d * DUO, (d + 1) * DUO):
+                nc.sync.dma_start(out=x_rows[t][:], in_=x_view[:, t, :])
 
-        nc.sync.dma_start(out=factors[:, 0, 1, :, :], in_=sin_view)
         load_x(0)
         for g in range(PASSES):
             nc.sync.dma_start(out=k_rows[g][:], in_=wk_view[g])
         load_x(1)
+        nc.sync.dma_start(out=factors[:, 0, 1, :, :], in_=sin_view)
         nc.sync.dma_start(out=factors[:, 0, 0, :, :], in_=cos_view)
         nc.sync.dma_start(out=factors[:, 1, 1, :, :], in_=cos_view)
         for d in range(2, DUOS):
@@ -133,33 +137,42 @@ def tile_groupedqueryattention_pa_kernel(
 
         make_identity(nc, identity[:])
         make_identity(nc, identity_bf16[:])
-        nc.gpsimd.tensor_scalar(
-            out=factors[:, 1, 0, :, :], in0=factors[:, 0, 1, :, :],
-            scalar1=-1.0, scalar2=0.0, op0=MULT, op1=ADD,
-        )
-
         pairs_of_identity = identity[:].rearrange("p (i e) -> p i e", e=2)
         pairs_of_swap = swap[:].rearrange("p (i e) -> p i e", e=2)
         for e in range(2):
-            nc.gpsimd.tensor_copy(out=pairs_of_swap[:, :, e], in_=pairs_of_identity[:, :, 1 - e])
+            nc.vector.tensor_copy(out=pairs_of_swap[:, :, e], in_=pairs_of_identity[:, :, 1 - e])
+        for a in range(2):
+            for o in range(2):
+                nc.vector.tensor_scalar(
+                    out=spreaders[:, a, :, :].rearrange("p e (i o) -> p (e i) o", o=2)[:, :, o],
+                    in0=identity_bf16[:],
+                    scalar1=-1.0 if (a == 1 and o == 1) else 1.0, scalar2=0.0, op0=MULT, op1=ADD,
+                )
 
-        def spread_factors():
-            flat_factors = factors[:].rearrange("p a e t i -> p (a e) (t i)")
-            nc.scalar.copy(
-                out=spread[:, 0, :, :].rearrange("p t (i e) -> p (t i) e", e=2),
-                in_=flat_factors[:, 0:4:3, :].rearrange("p z m -> p m z"),
-            )
-            nc.scalar.copy(
-                out=spread[:, 1, :, :].rearrange("p t (i e) -> p (t i) e", e=2),
-                in_=flat_factors[:, 1:3, :].rearrange("p z m -> p m z"),
-            )
-
-        def turn_factors():
+        def turn_pairs():
+            turned = banks.tile([P, 2 * BANK], BF16, tag="bank")
             for a in range(2):
-                turned = banks.tile([P, TILES * P], BF16, tag="bank")
-                for t in range(TILES):
-                    nc.tensor.transpose(turned[:, t * P : (t + 1) * P], spread[:, a, t, :], identity_bf16[:])
-                nc.scalar.copy(out=turned_factors[:, a, :, :].rearrange("p t n -> p (t n)"), in_=turned[:])
+                rows = factors[:, 0, a, :, :].rearrange("p t i -> p (t i)")
+                for u in range(TILES // 2):
+                    place = (a * (TILES // 2) + u) * P
+                    nc.tensor.transpose(turned[:, place : place + P], rows[:, u * P : (u + 1) * P], identity_bf16[:])
+            nc.scalar.copy(
+                out=pair_rows[:].rearrange("p a u n -> p (a u n)").bitcast(F32), in_=turned[:].bitcast(F32)
+            )
+
+        def spread_pairs(a):
+            spread = banks.tile([P, 2 * BANK], BF16, tag="bank")
+            for e in range(2):
+                nc.tensor.matmul(
+                    out=spread[:, e * BANK : (e + 1) * BANK],
+                    lhsT=spreaders[:, a, e, :],
+                    rhs=pair_rows[:, a, :, :].rearrange("p u n -> p (u n)"),
+                    start=True, stop=True,
+                )
+            nc.scalar.copy(
+                out=turned_factors[:, a, :, :].bitcast(F32).rearrange("p (u e) w -> p e u w", e=2),
+                in_=spread[:].bitcast(F32).rearrange("p (e u w) -> p e u w", e=2, w=P // 2),
+            )
 
         def project_turned(unit, h, tiles):
             sums = banks.tile([P, BANK], F32, tag="bank")
@@ -176,20 +189,18 @@ def tile_groupedqueryattention_pa_kernel(
                     )
             return sums
 
-        def rotate_turned(sums, tiles, result, on_gpsimd):
-            both = products.tile([P, 2, BANK], F32, tag="both")
-            engine = nc.vector
+        def rotate_turned(sums, tiles, on_gpsimd):
+            both = products.tile([P, 2, BANK], F32, tag="gboth" if on_gpsimd else "both", name="both_turned")
+            factor = turned_factors[:, :, tiles[0] : tiles[0] + len(tiles), :].rearrange("p a t n -> p a (t n)")
             if on_gpsimd:
                 copied = products.tile([P, BANK], F32, tag="copied")
                 nc.scalar.copy(out=copied[:], in_=sums[:])
-                sums = copied
-                engine = nc.gpsimd
-            engine.tensor_tensor(
-                out=both[:],
-                in0=sums[:].unsqueeze(1).to_broadcast([P, 2, BANK]),
-                in1=turned_factors[:, :, tiles[0] : tiles[0] + len(tiles), :].rearrange("p a t n -> p a (t n)"),
-                op=MULT,
-            )
+                for a in range(2):
+                    nc.gpsimd.tensor_tensor(out=both[:, a, :], in0=copied[:], in1=factor[:, a, :], op=MULT)
+            else:
+                nc.vector.tensor_tensor(
+                    out=both[:], in0=sums[:].unsqueeze(1).to_broadcast([P, 2, BANK]), in1=factor, op=MULT
+                )
             return both
 
         def turn_back(both, tiles, result):
@@ -208,7 +219,7 @@ def tile_groupedqueryattention_pa_kernel(
 
         def turn_x(t):
             d, s = divmod(t, DUO)
-            words = x_rows[d][:, s, :].bitcast(F32)
+            words = x_rows[t][:].bitcast(F32)
             turned = banks.tile([P, BANK], F32, tag="bank")
             for g in range(PASSES):
                 for u in range(2):
@@ -231,12 +242,15 @@ def tile_groupedqueryattention_pa_kernel(
                 in_=x_grouped[d][:].rearrange("p g s k -> p (g s k)"),
             )
 
+        def group_pass(unit, g, copy):
+            copy(
+                out=unit["grouped"][:, g, :, :].rearrange("p (c i) j -> p c j i", i=4),
+                in_=unit["rows"][g].rearrange("p j (c i) -> p c j i", i=4),
+            )
+
         def group_weights(unit, copy):
             for g in range(PASSES):
-                copy(
-                    out=unit["grouped"][:, g, :, :].rearrange("p (c i) j -> p c j i", i=4),
-                    in_=unit["rows"][g].rearrange("p j (c i) -> p c j i", i=4),
-                )
+                group_pass(unit, g, copy)
 
         def quantise_weights(unit):
             nc.vector.quantize_mx(
@@ -294,28 +308,17 @@ def tile_groupedqueryattention_pa_kernel(
             )
         for h in range(Q_HEADS):
             halves = [list(range(first, first + HALF_TILES)) for first in range(0, TILES, HALF_TILES)]
-            if h in SPLIT_HEADS:
-                for b, tiles in enumerate(halves):
-                    span = slice(tiles[0], tiles[0] + HALF_TILES)
-                    jobs.append(
-                        {
-                            "unit": q_units[h // UNIT_HEADS],
-                            "banks": [([h % UNIT_HEADS], tiles)],
-                            "adder": nc.vector if (h, b) in VECTOR_ADDS else nc.gpsimd,
-                            "turned": (h, b) in TURNED,
-                            "on_gpsimd": (h, b) in GPSIMD_MULTIPLIES,
-                            "out": q_result[h][:, span, :].rearrange("p (b t) f -> p b (t f)", b=1),
-                            "stores": [(q_view[:, h, span, :], q_result[h][:, span, :])],
-                        }
-                    )
-            else:
+            for b, tiles in enumerate(halves):
+                span = slice(tiles[0], tiles[0] + HALF_TILES)
                 jobs.append(
                     {
                         "unit": q_units[h // UNIT_HEADS],
-                        "banks": [([h % UNIT_HEADS], tiles) for tiles in halves],
-                        "adder": nc.gpsimd,
-                        "out": q_result[h][:].rearrange("p (b t) f -> p b (t f)", b=len(halves)),
-                        "stores": [(q_view[:, h, :, :], q_result[h][:])],
+                        "banks": [([h % UNIT_HEADS], tiles)],
+                        "adder": nc.vector if (h, b) in VECTOR_ADDS else nc.gpsimd,
+                        "turned": (h, b) in TURNED or (h, b) in ON_GPSIMD,
+                        "on_gpsimd": (h, b) in ON_GPSIMD,
+                        "out": q_result[h][:, span, :].rearrange("p (b t) f -> p b (t f)", b=1),
+                        "stores": [(q_view[:, h, span, :], q_result[h][:, span, :])],
                     }
                 )
         flat = [(j, b) for j, job in enumerate(jobs) for b in range(len(job["banks"]))]
@@ -337,11 +340,11 @@ def tile_groupedqueryattention_pa_kernel(
             heads, tiles = job["banks"][b]
             width = len(tiles) * HEAD
             if job.get("turned", False):
-                both = rotate_turned(sums_of[n], tiles, job["out"][:, 0, :], job["on_gpsimd"])
-                unfinished.append((both, tiles, job))
+                both = rotate_turned(sums_of[n], tiles, job["on_gpsimd"])
+                unfinished.append((n + (GPSIMD_DELAY if job["on_gpsimd"] else TURN_DELAY), both, tiles, job))
                 return
             if b == 0:
-                both_of[j] = products.tile([P, 2 * BANK // width, 2, width], F32, tag="both", name="both%d" % j)
+                both_of[j] = products.tile([P, BANK // width, 2, width], F32, tag="both", name="both%d" % j)
             for place, h in enumerate(heads):
                 multiply(sums_of[n], place * len(tiles), tiles, both_of[j][:, b * len(heads) + place, :, :])
                 if place == 0 and between is not None:
@@ -357,12 +360,13 @@ def tile_groupedqueryattention_pa_kernel(
                 for view, result in job["stores"]:
                     nc.sync.dma_start(out=view, in_=result)
 
-        def finish_turned():
-            for both, tiles, job in unfinished:
+        def finish_turned(n):
+            for entry in [e for e in unfinished if e[0] <= n]:
+                unfinished.remove(entry)
+                both, tiles, job = entry[1:]
                 turn_back(both, tiles, job["out"][:, 0, :])
                 for view, result in job["stores"]:
                     nc.sync.dma_start(out=view, in_=result)
-            unfinished.clear()
 
         def values(d):
             tiles = list(range(d * DUO, (d + 1) * DUO))
@@ -380,35 +384,41 @@ def tile_groupedqueryattention_pa_kernel(
         group_weights(k_unit, nc.vector.tensor_copy)
         quantise_weights(k_unit)
         quantise_x(0)
+        nc.vector.tensor_scalar(
+            out=factors[:, 1, 0, :, :], in0=factors[:, 0, 1, :, :],
+            scalar1=-1.0, scalar2=0.0, op0=MULT, op1=ADD,
+        )
         turn_x(2)
         turn_x(3)
         start_bank(0)
+        quantise_x(1)
+        rotate_bank(0)
         turn_x(4)
         turn_x(5)
-        quantise_x(1)
         start_bank(1)
-        rotate_bank(0)
+        quantise_x(2)
+        rotate_bank(1)
         turn_x(6)
         turn_x(7)
-        for unit in q_units + [v_unit]:
-            group_weights(unit, nc.scalar.copy)
-        quantise_x(2)
         start_bank(2)
-        rotate_bank(1)
         quantise_x(3)
-        start_bank(3)
         rotate_bank(2)
+        start_bank(3)
+        group_weights(q_units[0], nc.scalar.copy)
         quantise_weights(q_units[0])
+        group_weights(q_units[1], nc.scalar.copy)
         rotate_bank(3)
 
         started = DUOS
-        first_value_step = len(flat) - 2 * DUOS
+        first_value_step = 13
         quantised_units = 1
         for n in range(DUOS, len(flat)):
+            if BACK_FIRST:
+                finish_turned(n)
             while started <= min(n + LEAD, len(flat) - 1):
                 start_bank(started)
                 started += 1
-            finish_turned()
+            finish_turned(n)
             rotate_bank(n)
             ahead = min(n + LEAD + QUANT_AHEAD, len(flat) - 1)
             if quantised_units < Q_UNITS and jobs[flat[ahead][0]]["unit"] is q_units[quantised_units]:
@@ -416,9 +426,14 @@ def tile_groupedqueryattention_pa_kernel(
                 quantised_units += 1
             if n == first_value_step - 1:
                 quantise_weights(v_unit)
-            if n == TURN_STEP:
-                spread_factors()
-                turn_factors()
+            if n == DUOS:
+                turn_pairs()
+            if n == DUOS + 1:
+                for a in range(2):
+                    spread_pairs(a)
+            if n in GROUP_STEPS:
+                later, g = divmod(GROUP_STEPS.index(n), PASSES)
+                group_pass((q_units + [v_unit])[later + 2], g, nc.scalar.copy)
             if first_value_step <= n < first_value_step + DUOS:
                 values(n - first_value_step)
-        finish_turned()
+        finish_turned(len(flat) + GPSIMD_DELAY)

@@ -31,6 +31,9 @@ Q_LOAD_UNITS = 2
 WORDS = K_PASS // 2
 HALF_TILES = BANK // HEAD
 GROUP_STEPS = (6, 7, 8, 9, 10, 11)
+GROUP_ORDER = (2, 4, 3)
+VALUE_QUANT_STEP = 10
+VALUE_STEPS = (11, 12, 13, 14)
 LEAD = 2
 QUANT_AHEAD = 1
 TURNED = ((2,0),(4,0),(6,0))
@@ -38,6 +41,7 @@ ON_GPSIMD = ()
 TURN_DELAY = 1
 BACK_FIRST = True
 GPSIMD_DELAY = 3
+KEY_VECTOR_ADDS = (0,)
 VECTOR_ADDS = ((7, 1),)
 
 FLOPS = 2 * TOKENS * FEATURES * (Q_HEADS + 2 * UNIT_HEADS) * HEAD
@@ -56,9 +60,9 @@ def tile_groupedqueryattention_pa_kernel(
         x_view = x[0].rearrange("(p t) k -> p t k", t=TILES)
         cos_view = rope_cos[0].rearrange("(p t) i -> p t i", t=TILES)
         sin_view = rope_sin[0].rearrange("(p t) i -> p t i", t=TILES)
-        wq_view = Wq.rearrange("(g p j) c -> g p j c", g=PASSES, j=PACK)
-        wk_view = Wk.rearrange("(g p j) c -> g p j c", g=PASSES, j=PACK)
-        wv_view = Wv.rearrange("(g p j) c -> g p j c", g=PASSES, j=PACK)
+        wq_view = Wq.rearrange("(g u p e) c -> g u p e c", g=PASSES, u=2, e=2)
+        wk_view = Wk.rearrange("(g u p e) c -> g p u (e c)", g=PASSES, u=2, e=2)
+        wv_view = Wv.rearrange("(g u p e) c -> g p u (e c)", g=PASSES, u=2, e=2)
         q_view = out_0[0].rearrange("h (p t) d -> p h t d", t=TILES)
         k_view = out_1[0].rearrange("h (p t) d -> p h t d", t=TILES)
         v_view = out_2[0].rearrange("h (p t) d -> p h t d", t=TILES)
@@ -121,7 +125,7 @@ def tile_groupedqueryattention_pa_kernel(
 
         load_x(0)
         for g in range(PASSES):
-            nc.sync.dma_start(out=k_rows[g][:], in_=wk_view[g])
+            nc.sync.dma_start(out=k_rows[g][:].rearrange("p (u e) c -> p u (e c)", u=2), in_=wk_view[g])
         load_x(1)
         nc.sync.dma_start(out=factors[:, 0, 1, :, :], in_=sin_view)
         nc.sync.dma_start(out=factors[:, 0, 0, :, :], in_=cos_view)
@@ -131,9 +135,12 @@ def tile_groupedqueryattention_pa_kernel(
         for part in range(Q_UNITS // Q_LOAD_UNITS):
             cols = slice(part * Q_LOAD_UNITS * UNIT_COLS, (part + 1) * Q_LOAD_UNITS * UNIT_COLS)
             for g in range(PASSES):
-                nc.sync.dma_start(out=q_rows[part][g][:], in_=wq_view[g, :, :, cols])
+                for u in range(2):
+                    nc.sync.dma_start(
+                        out=q_rows[part][g][:, 2 * u : 2 * u + 2, :], in_=wq_view[g, u, :, :, cols]
+                    )
         for g in range(PASSES):
-            nc.sync.dma_start(out=v_rows[g][:], in_=wv_view[g])
+            nc.sync.dma_start(out=v_rows[g][:].rearrange("p (u e) c -> p u (e c)", u=2), in_=wv_view[g])
 
         make_identity(nc, identity[:])
         make_identity(nc, identity_bf16[:])
@@ -223,11 +230,11 @@ def tile_groupedqueryattention_pa_kernel(
             turned = banks.tile([P, BANK], F32, tag="bank")
             for g in range(PASSES):
                 for u in range(2):
-                    first = g * WORDS + u
+                    first = g * WORDS + u * P
                     piece = (g * 2 + u) * P
                     nc.tensor.transpose(
                         turned[:, piece : piece + P],
-                        words[:, first : (g + 1) * WORDS : 2],
+                        words[:, first : first + P],
                         identity[:],
                     )
             nc.scalar.copy(
@@ -298,7 +305,7 @@ def tile_groupedqueryattention_pa_kernel(
                 {
                     "unit": k_unit,
                     "banks": [(list(range(UNIT_HEADS)), tiles)],
-                    "adder": nc.gpsimd,
+                    "adder": nc.vector if d in KEY_VECTOR_ADDS else nc.gpsimd,
                     "out": k_result[:, :, tiles[0] : tiles[0] + DUO, :].rearrange("p h t f -> p h (t f)"),
                     "stores": [
                         (k_view[:, :, tiles[0] - DUO : tiles[0] + DUO, :],
@@ -395,11 +402,11 @@ def tile_groupedqueryattention_pa_kernel(
         rotate_bank(0)
         turn_x(4)
         turn_x(5)
+        turn_x(6)
+        turn_x(7)
         start_bank(1)
         quantise_x(2)
         rotate_bank(1)
-        turn_x(6)
-        turn_x(7)
         start_bank(2)
         quantise_x(3)
         rotate_bank(2)
@@ -410,7 +417,6 @@ def tile_groupedqueryattention_pa_kernel(
         rotate_bank(3)
 
         started = DUOS
-        first_value_step = 13
         quantised_units = 1
         for n in range(DUOS, len(flat)):
             if BACK_FIRST:
@@ -424,7 +430,7 @@ def tile_groupedqueryattention_pa_kernel(
             if quantised_units < Q_UNITS and jobs[flat[ahead][0]]["unit"] is q_units[quantised_units]:
                 quantise_weights(q_units[quantised_units])
                 quantised_units += 1
-            if n == first_value_step - 1:
+            if n == VALUE_QUANT_STEP:
                 quantise_weights(v_unit)
             if n == DUOS:
                 turn_pairs()
@@ -433,7 +439,7 @@ def tile_groupedqueryattention_pa_kernel(
                     spread_pairs(a)
             if n in GROUP_STEPS:
                 later, g = divmod(GROUP_STEPS.index(n), PASSES)
-                group_pass((q_units + [v_unit])[later + 2], g, nc.scalar.copy)
-            if first_value_step <= n < first_value_step + DUOS:
-                values(n - first_value_step)
+                group_pass((q_units + [v_unit])[GROUP_ORDER[later]], g, nc.scalar.copy)
+            if n in VALUE_STEPS:
+                values(VALUE_STEPS.index(n))
         finish_turned(len(flat) + GPSIMD_DELAY)

@@ -32,8 +32,8 @@ WORDS = K_PASS // 2
 HALF_TILES = BANK // HEAD
 GROUP_STEPS = (6, 7, 8, 9, 10, 11)
 GROUP_ORDER = (2, 4, 3)
-VALUE_QUANT_STEP = 10
-VALUE_STEPS = (11, 12, 13, 14)
+VALUE_QUANT_STEP = 11
+VALUE_STEPS = (12,13,14,15)
 LEAD = 2
 QUANT_AHEAD = 1
 TURNED = ((2,0),(4,0),(6,0))
@@ -41,7 +41,7 @@ ON_GPSIMD = ()
 TURN_DELAY = 1
 BACK_FIRST = True
 GPSIMD_DELAY = 3
-KEY_VECTOR_ADDS = (0,)
+KEY_VECTOR_ADDS = ()
 VECTOR_ADDS = ((7, 1),)
 
 FLOPS = 2 * TOKENS * FEATURES * (Q_HEADS + 2 * UNIT_HEADS) * HEAD
@@ -53,7 +53,7 @@ def tile_groupedqueryattention_pa_kernel(
     nc = tc.nc
     with ExitStack() as stack:
         keep = stack.enter_context(tc.tile_pool(name="keep", bufs=1))
-        products = stack.enter_context(tc.tile_pool(name="products", bufs=5))
+        products = stack.enter_context(tc.tile_pool(name="products", bufs=17))
         banks = stack.enter_context(tc.psum_pool(name="banks", bufs=8))
         stack.enter_context(tc.manual_schedule())
 
@@ -389,8 +389,8 @@ def tile_groupedqueryattention_pa_kernel(
         turn_x(0)
         turn_x(1)
         group_weights(k_unit, nc.vector.tensor_copy)
-        quantise_weights(k_unit)
         quantise_x(0)
+        quantise_weights(k_unit)
         nc.vector.tensor_scalar(
             out=factors[:, 1, 0, :, :], in0=factors[:, 0, 1, :, :],
             scalar1=-1.0, scalar2=0.0, op0=MULT, op1=ADD,

@@ -36,7 +36,7 @@ VALUE_QUANT_STEP = 11
 VALUE_STEPS = (12,13,14,15)
 LEAD = 2
 QUANT_AHEAD = 1
-TURNED = ((2,0),(4,0),(6,0))
+TURNED = ((2,0),(4,0),(6,1))
 ON_GPSIMD = ()
 TURN_DELAY = 1
 BACK_FIRST = True
@@ -129,7 +129,6 @@ def tile_groupedqueryattention_pa_kernel(
         load_x(1)
         nc.sync.dma_start(out=factors[:, 0, 1, :, :], in_=sin_view)
         nc.sync.dma_start(out=factors[:, 0, 0, :, :], in_=cos_view)
-        nc.sync.dma_start(out=factors[:, 1, 1, :, :], in_=cos_view)
         for d in range(2, DUOS):
             load_x(d)
         for part in range(Q_UNITS // Q_LOAD_UNITS):
@@ -142,6 +141,8 @@ def tile_groupedqueryattention_pa_kernel(
         for g in range(PASSES):
             nc.sync.dma_start(out=v_rows[g][:].rearrange("p (u e) c -> p u (e c)", u=2), in_=wv_view[g])
 
+        zeros = keep.tile([P, P], BF16)
+        nc.vector.memset(zeros[:], 0.0)
         make_identity(nc, identity[:])
         make_identity(nc, identity_bf16[:])
         pairs_of_identity = identity[:].rearrange("p (i e) -> p i e", e=2)
@@ -223,6 +224,11 @@ def tile_groupedqueryattention_pa_kernel(
                     is_transpose=True, start=False, stop=True,
                 )
             nc.scalar.copy(out=result, in_=rotated[:])
+
+        def keep_clock(moving, count):
+            for i in range(count):
+                unread = banks.tile([P, BANK], F32, tag="bank", name="unread")
+                nc.tensor.matmul(out=unread[:], lhsT=zeros[:], rhs=moving, start=True, stop=True)
 
         def turn_x(t):
             d, s = divmod(t, DUO)
@@ -386,11 +392,15 @@ def tile_groupedqueryattention_pa_kernel(
                 span = slice(tiles[0] - DUO, tiles[0] + DUO)
                 nc.sync.dma_start(out=v_view[:, :, span, :], in_=v_result[:, :, span, :])
 
+        keep_clock(zeros[:, 0:1].to_broadcast([P, BANK]), 0)
         turn_x(0)
         turn_x(1)
+        for g in range(PASSES):
+            keep_clock(k_rows[g][:, 0:2, :].rearrange("p j c -> p (j c)"), 2)
         group_weights(k_unit, nc.vector.tensor_copy)
         quantise_x(0)
         quantise_weights(k_unit)
+        nc.vector.tensor_copy(out=factors[:, 1, 1, :, :], in_=factors[:, 0, 0, :, :])
         nc.vector.tensor_scalar(
             out=factors[:, 1, 0, :, :], in0=factors[:, 0, 1, :, :],
             scalar1=-1.0, scalar2=0.0, op0=MULT, op1=ADD,

@@ -30,10 +30,10 @@ Q_UNITS = Q_HEADS // UNIT_HEADS
 Q_LOAD_UNITS = 2
 WORDS = K_PASS // 2
 HALF_TILES = BANK // HEAD
-GROUP_STEPS = (6, 7, 8, 9, 10, 11)
+GROUP_STEPS = (4,5,6,7,8,9)
 GROUP_ORDER = (2, 4, 3)
-VALUE_QUANT_STEP = 11
-VALUE_STEPS = (12,13,14,15)
+VALUE_QUANT_STEP = 10
+VALUE_STEPS = (11,12,13,14)
 LEAD = 2
 QUANT_AHEAD = 1
 TURNED = ((2,0),(4,0),(6,1))
@@ -392,11 +392,10 @@ def tile_groupedqueryattention_pa_kernel(
                 span = slice(tiles[0] - DUO, tiles[0] + DUO)
                 nc.sync.dma_start(out=v_view[:, :, span, :], in_=v_result[:, :, span, :])
 
-        keep_clock(zeros[:, 0:1].to_broadcast([P, BANK]), 0)
         turn_x(0)
         turn_x(1)
         for g in range(PASSES):
-            keep_clock(k_rows[g][:, 0:2, :].rearrange("p j c -> p (j c)"), 2)
+            keep_clock(k_rows[g][:, 0:2, :].rearrange("p j c -> p (j c)"), 1)
         group_weights(k_unit, nc.vector.tensor_copy)
         quantise_x(0)
         quantise_weights(k_unit)
@@ -422,6 +421,7 @@ def tile_groupedqueryattention_pa_kernel(
         rotate_bank(2)
         start_bank(3)
         group_weights(q_units[0], nc.scalar.copy)
+        turn_pairs()
         quantise_weights(q_units[0])
         group_weights(q_units[1], nc.scalar.copy)
         rotate_bank(3)
@@ -443,8 +443,6 @@ def tile_groupedqueryattention_pa_kernel(
             if n == VALUE_QUANT_STEP:
                 quantise_weights(v_unit)
             if n == DUOS:
-                turn_pairs()
-            if n == DUOS + 1:
                 for a in range(2):
                     spread_pairs(a)
             if n in GROUP_STEPS:

@@ -27,7 +27,7 @@ UNIT_COLS = UNIT_HEADS * HEAD
 DUO = 2
 DUOS = TILES // DUO
 Q_UNITS = Q_HEADS // UNIT_HEADS
-Q_LOAD_UNITS = 2
+Q_LOADS = ((0, 1), (1, 2), (2, 4))
 WORDS = K_PASS // 2
 HALF_TILES = BANK // HEAD
 GROUP_STEPS = (4,5,6,7,8,9)
@@ -41,7 +41,7 @@ ON_GPSIMD = ()
 TURN_DELAY = 1
 BACK_FIRST = True
 GPSIMD_DELAY = 3
-KEY_VECTOR_ADDS = ()
+KEY_VECTOR_ADDS = (1,)
 VECTOR_ADDS = ((7, 1),)
 
 FLOPS = 2 * TOKENS * FEATURES * (Q_HEADS + 2 * UNIT_HEADS) * HEAD
@@ -85,10 +85,10 @@ def tile_groupedqueryattention_pa_kernel(
         v_rows = [keep.tile([P, PACK, UNIT_COLS], BF16, name="v_rows%d" % g) for g in range(PASSES)]
         q_rows = [
             [
-                keep.tile([P, PACK, Q_LOAD_UNITS * UNIT_COLS], BF16, name="q_rows%d_%d" % (part, g))
+                keep.tile([P, PACK, (last - first) * UNIT_COLS], BF16, name="q_rows%d_%d" % (first, g))
                 for g in range(PASSES)
             ]
-            for part in range(Q_UNITS // Q_LOAD_UNITS)
+            for first, last in Q_LOADS
         ]
 
         def weight_unit(name, rows_of_pass):
@@ -104,10 +104,12 @@ def tile_groupedqueryattention_pa_kernel(
         k_unit = weight_unit("k", [rows[:] for rows in k_rows])
         v_unit = weight_unit("v", [rows[:] for rows in v_rows])
         q_units = []
-        for u in range(Q_UNITS):
-            part, place = divmod(u, Q_LOAD_UNITS)
-            cols = slice(place * UNIT_COLS, (place + 1) * UNIT_COLS)
-            q_units.append(weight_unit("q%d" % u, [q_rows[part][g][:, :, cols] for g in range(PASSES)]))
+        for (first, last), rows in zip(Q_LOADS, q_rows):
+            for place in range(last - first):
+                cols = slice(place * UNIT_COLS, (place + 1) * UNIT_COLS)
+                q_units.append(
+                    weight_unit("q%d" % (first + place), [rows[g][:, :, cols] for g in range(PASSES)])
+                )
 
         factors = keep.tile([P, 2, 2, TILES, PAIRS], BF16)
         identity_bf16 = keep.tile([P, P], BF16)
@@ -129,15 +131,16 @@ def tile_groupedqueryattention_pa_kernel(
         load_x(1)
         nc.sync.dma_start(out=factors[:, 0, 1, :, :], in_=sin_view)
         nc.sync.dma_start(out=factors[:, 0, 0, :, :], in_=cos_view)
-        for d in range(2, DUOS):
-            load_x(d)
-        for part in range(Q_UNITS // Q_LOAD_UNITS):
-            cols = slice(part * Q_LOAD_UNITS * UNIT_COLS, (part + 1) * Q_LOAD_UNITS * UNIT_COLS)
+        for part, (first, last) in enumerate(Q_LOADS):
+            cols = slice(first * UNIT_COLS, last * UNIT_COLS)
             for g in range(PASSES):
                 for u in range(2):
                     nc.sync.dma_start(
                         out=q_rows[part][g][:, 2 * u : 2 * u + 2, :], in_=wq_view[g, u, :, :, cols]
                     )
+            if part == 0:
+                for d in range(2, DUOS):
+                    load_x(d)
         for g in range(PASSES):
             nc.sync.dma_start(out=v_rows[g][:].rearrange("p (u e) c -> p u (e c)", u=2), in_=wv_view[g])
 
@@ -334,6 +337,8 @@ def tile_groupedqueryattention_pa_kernel(
                         "stores": [(q_view[:, h, span, :], q_result[h][:, span, :])],
                     }
                 )
+        keys_behind, first_queries = jobs[2:DUOS], jobs[DUOS : DUOS + 2 * UNIT_HEADS]
+        jobs[2 : DUOS + 2 * UNIT_HEADS] = first_queries[0::2] + keys_behind + first_queries[1::2]
         flat = [(j, b) for j, job in enumerate(jobs) for b in range(len(job["banks"]))]
         sums_of = {}
         both_of = {}
@@ -347,7 +352,7 @@ def tile_groupedqueryattention_pa_kernel(
             else:
                 sums_of[n] = project(jobs[j]["unit"], heads, tiles)
 
-        def rotate_bank(n, between=None):
+        def rotate_bank(n, between=None, before_add=None):
             j, b = flat[n]
             job = jobs[j]
             heads, tiles = job["banks"][b]
@@ -364,6 +369,8 @@ def tile_groupedqueryattention_pa_kernel(
                     between()
             if b == len(job["banks"]) - 1:
                 used = len(job["banks"]) * len(heads)
+                if before_add is not None:
+                    before_add()
                 job["adder"].tensor_tensor(
                     out=job["out"],
                     in0=both_of[j][:, 0:used, 0, :],
@@ -409,24 +416,25 @@ def tile_groupedqueryattention_pa_kernel(
         start_bank(0)
         quantise_x(1)
         rotate_bank(0)
+        start_bank(1)
+        group_weights(q_units[0], nc.scalar.copy)
         turn_x(4)
         turn_x(5)
+        keep_clock(x_rows[5][:, 0:BANK], 2)
+        rotate_bank(1, before_add=lambda: quantise_weights(q_units[0]))
+        start_bank(2)
+        start_bank(3)
         turn_x(6)
         turn_x(7)
-        start_bank(1)
-        quantise_x(2)
-        rotate_bank(1)
-        start_bank(2)
-        quantise_x(3)
-        rotate_bank(2)
-        start_bank(3)
-        group_weights(q_units[0], nc.scalar.copy)
         turn_pairs()
-        quantise_weights(q_units[0])
+        quantise_x(2)
+        rotate_bank(2)
+        start_bank(4)
         group_weights(q_units[1], nc.scalar.copy)
         rotate_bank(3)
+        quantise_x(3)
 
-        started = DUOS
+        started = DUOS + 1
         quantised_units = 1
         for n in range(DUOS, len(flat)):
             if BACK_FIRST:

from contextlib import ExitStack

import concourse.mybir as mybir
from concourse.masks import make_identity

F32 = mybir.dt.float32
BF16 = mybir.dt.bfloat16
U32 = mybir.dt.uint32
U8 = mybir.dt.uint8
FP8X4 = mybir.dt.float8_e4m3fn_x4
MULT = mybir.AluOpType.mult
ADD = mybir.AluOpType.add

P = 128
PACK = 4
K_PASS = P * PACK
TOKENS = 1024
FEATURES = 1024
PASSES = FEATURES // K_PASS
TILES = TOKENS // P
HEAD = 128
PAIRS = HEAD // 2
BANK = 512
Q_HEADS = 8
UNIT_HEADS = 2
UNIT_COLS = UNIT_HEADS * HEAD
DUO = 2
DUOS = TILES // DUO
Q_UNITS = Q_HEADS // UNIT_HEADS
Q_LOADS = ((0, 1), (1, 2), (2, 4))
WORDS = K_PASS // 2
HALF_TILES = BANK // HEAD
GROUP_STEPS = (4,5,6,7,8,9)
GROUP_ORDER = (2, 4, 3)
VALUE_QUANT_STEP = 10
VALUE_STEPS = (11,12,13,14)
LEAD = 2
QUANT_AHEAD = 1
TURNED = ((2,0),(4,0),(6,1))
ON_GPSIMD = ()
TURN_DELAY = 1
BACK_FIRST = True
GPSIMD_DELAY = 3
KEY_VECTOR_ADDS = (1,)
VECTOR_ADDS = ((7, 1),)

FLOPS = 2 * TOKENS * FEATURES * (Q_HEADS + 2 * UNIT_HEADS) * HEAD


def tile_groupedqueryattention_pa_kernel(
    tc, x, rope_cos, rope_sin, Wq, Wk, Wv, out_0, out_1, out_2
):
    nc = tc.nc
    with ExitStack() as stack:
        keep = stack.enter_context(tc.tile_pool(name="keep", bufs=1))
        products = stack.enter_context(tc.tile_pool(name="products", bufs=17))
        banks = stack.enter_context(tc.psum_pool(name="banks", bufs=8))
        stack.enter_context(tc.manual_schedule())

        x_view = x[0].rearrange("(p t) k -> p t k", t=TILES)
        cos_view = rope_cos[0].rearrange("(p t) i -> p t i", t=TILES)
        sin_view = rope_sin[0].rearrange("(p t) i -> p t i", t=TILES)
        wq_view = Wq.rearrange("(g u p e) c -> g u p e c", g=PASSES, u=2, e=2)
        wk_view = Wk.rearrange("(g u p e) c -> g p u (e c)", g=PASSES, u=2, e=2)
        wv_view = Wv.rearrange("(g u p e) c -> g p u (e c)", g=PASSES, u=2, e=2)
        q_view = out_0[0].rearrange("h (p t) d -> p h t d", t=TILES)
        k_view = out_1[0].rearrange("h (p t) d -> p h t d", t=TILES)
        v_view = out_2[0].rearrange("h (p t) d -> p h t d", t=TILES)

        identity = keep.tile([P, P], F32)
        x_rows = [keep.tile([P, FEATURES], BF16, name="x_rows%d" % t) for t in range(TILES)]
        x_grouped = [
            keep.tile([P, PASSES, DUO, K_PASS], BF16, name="x_grouped%d" % d, align_bytes=64)
            for d in range(DUOS)
        ]
        x_codes = [
            keep.tile([P, PASSES, DUO, P], U32, name="x_codes%d" % d, align_bytes=64)
            for d in range(DUOS)
        ]
        x_scales = [
            keep.tile([P, PASSES, DUO, P], U8, name="x_scales%d" % d, align_bytes=64)
            for d in range(DUOS)
        ]
        k_rows = [keep.tile([P, PACK, UNIT_COLS], BF16, name="k_rows%d" % g) for g in range(PASSES)]
        v_rows = [keep.tile([P, PACK, UNIT_COLS], BF16, name="v_rows%d" % g) for g in range(PASSES)]
        q_rows = [
            [
                keep.tile([P, PACK, (last - first) * UNIT_COLS], BF16, name="q_rows%d_%d" % (first, g))
                for g in range(PASSES)
            ]
            for first, last in Q_LOADS
        ]

        def weight_unit(name, rows_of_pass):
            return {
                "rows": rows_of_pass,
                "grouped": keep.tile(
                    [P, PASSES, UNIT_COLS, PACK], BF16, name="grouped_" + name, align_bytes=64
                ),
                "codes": keep.tile([P, PASSES, UNIT_COLS], U32, name="codes_" + name, align_bytes=64),
                "scales": keep.tile([P, PASSES, UNIT_COLS], U8, name="scales_" + name, align_bytes=64),
            }

        k_unit = weight_unit("k", [rows[:] for rows in k_rows])
        v_unit = weight_unit("v", [rows[:] for rows in v_rows])
        q_units = []
        for (first, last), rows in zip(Q_LOADS, q_rows):
            for place in range(last - first):
                cols = slice(place * UNIT_COLS, (place + 1) * UNIT_COLS)
                q_units.append(
                    weight_unit("q%d" % (first + place), [rows[g][:, :, cols] for g in range(PASSES)])
                )

        factors = keep.tile([P, 2, 2, TILES, PAIRS], BF16)
        identity_bf16 = keep.tile([P, P], BF16)
        swap = keep.tile([P, P], F32)
        spreaders = keep.tile([P, 2, 2, HEAD], BF16)
        pair_rows = keep.tile([P, 2, TILES // 2, P], BF16)
        turned_factors = keep.tile([P, 2, TILES, P], BF16)
        k_result = keep.tile([P, UNIT_HEADS, TILES, HEAD], F32)
        v_result = keep.tile([P, UNIT_HEADS, TILES, HEAD], F32)
        q_result = [keep.tile([P, TILES, HEAD], F32, name="q_result%d" % h) for h in range(Q_HEADS)]

        def load_x(d):
            for t in range(d * DUO, (d + 1) * DUO):
                nc.sync.dma_start(out=x_rows[t][:], in_=x_view[:, t, :])

        load_x(0)
        for g in range(PASSES):
            nc.sync.dma_start(out=k_rows[g][:].rearrange("p (u e) c -> p u (e c)", u=2), in_=wk_view[g])
        load_x(1)
        nc.sync.dma_start(out=factors[:, 0, 1, :, :], in_=sin_view)
        nc.sync.dma_start(out=factors[:, 0, 0, :, :], in_=cos_view)
        for part, (first, last) in enumerate(Q_LOADS):
            cols = slice(first * UNIT_COLS, last * UNIT_COLS)
            for g in range(PASSES):
                for u in range(2):
                    nc.sync.dma_start(
                        out=q_rows[part][g][:, 2 * u : 2 * u + 2, :], in_=wq_view[g, u, :, :, cols]
                    )
            if part == 0:
                for d in range(2, DUOS):
                    load_x(d)
        for g in range(PASSES):
            nc.sync.dma_start(out=v_rows[g][:].rearrange("p (u e) c -> p u (e c)", u=2), in_=wv_view[g])

        zeros = keep.tile([P, P], BF16)
        nc.vector.memset(zeros[:], 0.0)
        make_identity(nc, identity[:])
        make_identity(nc, identity_bf16[:])
        pairs_of_identity = identity[:].rearrange("p (i e) -> p i e", e=2)
        pairs_of_swap = swap[:].rearrange("p (i e) -> p i e", e=2)
        for e in range(2):
            nc.vector.tensor_copy(out=pairs_of_swap[:, :, e], in_=pairs_of_identity[:, :, 1 - e])
        for a in range(2):
            for o in range(2):
                nc.vector.tensor_scalar(
                    out=spreaders[:, a, :, :].rearrange("p e (i o) -> p (e i) o", o=2)[:, :, o],
                    in0=identity_bf16[:],
                    scalar1=-1.0 if (a == 1 and o == 1) else 1.0, scalar2=0.0, op0=MULT, op1=ADD,
                )

        def turn_pairs():
            turned = banks.tile([P, 2 * BANK], BF16, tag="bank")
            for a in range(2):
                rows = factors[:, 0, a, :, :].rearrange("p t i -> p (t i)")
                for u in range(TILES // 2):
                    place = (a * (TILES // 2) + u) * P
                    nc.tensor.transpose(turned[:, place : place + P], rows[:, u * P : (u + 1) * P], identity_bf16[:])
            nc.scalar.copy(
                out=pair_rows[:].rearrange("p a u n -> p (a u n)").bitcast(F32), in_=turned[:].bitcast(F32)
            )

        def spread_pairs(a):
            spread = banks.tile([P, 2 * BANK], BF16, tag="bank")
            for e in range(2):
                nc.tensor.matmul(
                    out=spread[:, e * BANK : (e + 1) * BANK],
                    lhsT=spreaders[:, a, e, :],
                    rhs=pair_rows[:, a, :, :].rearrange("p u n -> p (u n)"),
                    start=True, stop=True,
                )
            nc.scalar.copy(
                out=turned_factors[:, a, :, :].bitcast(F32).rearrange("p (u e) w -> p e u w", e=2),
                in_=spread[:].bitcast(F32).rearrange("p (e u w) -> p e u w", e=2, w=P // 2),
            )

        def project_turned(unit, h, tiles):
            sums = banks.tile([P, BANK], F32, tag="bank")
            for place, d in enumerate(range(tiles[0] // DUO, tiles[0] // DUO + len(tiles) // DUO)):
                for g in range(PASSES):
                    nc.tensor.matmul_mx(
                        out=sums[:, place * DUO * P : (place + 1) * DUO * P],
                        lhsT=unit["codes"][:, g, h * HEAD : (h + 1) * HEAD].bitcast(FP8X4),
                        lhsT_scale=unit["scales"][:, g, h * HEAD : (h + 1) * HEAD],
                        rhs=x_codes[d][:, g, :, :].rearrange("p s n -> p (s n)").bitcast(FP8X4),
                        rhs_scale=x_scales[d][:, g, :, :].rearrange("p s n -> p (s n)"),
                        start=(g == 0),
                        stop=(g == PASSES - 1),
                    )
            return sums

        def rotate_turned(sums, tiles, on_gpsimd):
            both = products.tile([P, 2, BANK], F32, tag="gboth" if on_gpsimd else "both", name="both_turned")
            factor = turned_factors[:, :, tiles[0] : tiles[0] + len(tiles), :].rearrange("p a t n -> p a (t n)")
            if on_gpsimd:
                copied = products.tile([P, BANK], F32, tag="copied")
                nc.scalar.copy(out=copied[:], in_=sums[:])
                for a in range(2):
                    nc.gpsimd.tensor_tensor(out=both[:, a, :], in0=copied[:], in1=factor[:, a, :], op=MULT)
            else:
                nc.vector.tensor_tensor(
                    out=both[:], in0=sums[:].unsqueeze(1).to_broadcast([P, 2, BANK]), in1=factor, op=MULT
                )
            return both

        def turn_back(both, tiles, result):
            rotated = banks.tile([P, BANK], F32, tag="bank")
            for place in range(len(tiles)):
                cols = slice(place * P, (place + 1) * P)
                nc.tensor.matmul(
                    out=rotated[:, cols], lhsT=both[:, 0, cols], rhs=identity[:],
                    is_transpose=True, start=True, stop=False,
                )
                nc.tensor.matmul(
                    out=rotated[:, cols], lhsT=both[:, 1, cols], rhs=swap[:],
                    is_transpose=True, start=False, stop=True,
                )
            nc.scalar.copy(out=result, in_=rotated[:])

        def keep_clock(moving, count):
            for i in range(count):
                unread = banks.tile([P, BANK], F32, tag="bank", name="unread")
                nc.tensor.matmul(out=unread[:], lhsT=zeros[:], rhs=moving, start=True, stop=True)

        def turn_x(t):
            d, s = divmod(t, DUO)
            words = x_rows[t][:].bitcast(F32)
            turned = banks.tile([P, BANK], F32, tag="bank")
            for g in range(PASSES):
                for u in range(2):
                    first = g * WORDS + u * P
                    piece = (g * 2 + u) * P
                    nc.tensor.transpose(
                        turned[:, piece : piece + P],
                        words[:, first : first + P],
                        identity[:],
                    )
            nc.scalar.copy(
                out=x_grouped[d][:, :, s, :].bitcast(F32).rearrange("p g (n u) -> p g n u", u=2),
                in_=turned[:].rearrange("p (g u n) -> p g n u", g=PASSES, u=2),
            )

        def quantise_x(d):
            nc.vector.quantize_mx(
                out=x_codes[d][:].rearrange("p g s n -> p (g s n)").bitcast(FP8X4),
                scales=x_scales[d][:].rearrange("p g s n -> p (g s n)"),
                in_=x_grouped[d][:].rearrange("p g s k -> p (g s k)"),
            )

        def group_pass(unit, g, copy):
            copy(
                out=unit["grouped"][:, g, :, :].rearrange("p (c i) j -> p c j i", i=4),
                in_=unit["rows"][g].rearrange("p j (c i) -> p c j i", i=4),
            )

        def group_weights(unit, copy):
            for g in range(PASSES):
                group_pass(unit, g, copy)

        def quantise_weights(unit):
            nc.vector.quantize_mx(
                out=unit["codes"][:].rearrange("p g c -> p (g c)").bitcast(FP8X4),
                scales=unit["scales"][:].rearrange("p g c -> p (g c)"),
                in_=unit["grouped"][:].rearrange("p g c j -> p (g c j)"),
            )

        def project(unit, heads, tiles):
            sums = banks.tile([P, BANK], F32, tag="bank")
            place = 0
            for h in heads:
                for t in tiles:
                    d, s = divmod(t, DUO)
                    for g in range(PASSES):
                        nc.tensor.matmul_mx(
                            out=sums[:, place * HEAD : (place + 1) * HEAD],
                            lhsT=x_codes[d][:, g, s, :].bitcast(FP8X4),
                            lhsT_scale=x_scales[d][:, g, s, :],
                            rhs=unit["codes"][:, g, h * HEAD : (h + 1) * HEAD].bitcast(FP8X4),
                            rhs_scale=unit["scales"][:, g, h * HEAD : (h + 1) * HEAD],
                            start=(g == 0),
                            stop=(g == PASSES - 1),
                        )
                    place += 1
            return sums

        def multiply(sums, place, tiles, both):
            width = len(tiles) * HEAD
            shape = [P, 2, width // 2, 2]
            y = sums[:, place * HEAD : place * HEAD + width].rearrange("p (m a) -> p a m", a=2)
            nc.vector.tensor_tensor(
                out=both.rearrange("p a (m e) -> p a m e", e=2),
                in0=y.unsqueeze(3).to_broadcast(shape),
                in1=factors[:, :, :, tiles[0] : tiles[0] + len(tiles), :].rearrange(
                    "p a e t i -> p a (t i) e"
                ),
                op=MULT,
            )

        jobs = []
        for d in range(DUOS):
            tiles = list(range(d * DUO, (d + 1) * DUO))
            jobs.append(
                {
                    "unit": k_unit,
                    "banks": [(list(range(UNIT_HEADS)), tiles)],
                    "adder": nc.vector if d in KEY_VECTOR_ADDS else nc.gpsimd,
                    "out": k_result[:, :, tiles[0] : tiles[0] + DUO, :].rearrange("p h t f -> p h (t f)"),
                    "stores": [
                        (k_view[:, :, tiles[0] - DUO : tiles[0] + DUO, :],
                         k_result[:, :, tiles[0] - DUO : tiles[0] + DUO, :])
                    ] if d % 2 == 1 else [],
                }
            )
        for h in range(Q_HEADS):
            halves = [list(range(first, first + HALF_TILES)) for first in range(0, TILES, HALF_TILES)]
            for b, tiles in enumerate(halves):
                span = slice(tiles[0], tiles[0] + HALF_TILES)
                jobs.append(
                    {
                        "unit": q_units[h // UNIT_HEADS],
                        "banks": [([h % UNIT_HEADS], tiles)],
                        "adder": nc.vector if (h, b) in VECTOR_ADDS else nc.gpsimd,
                        "turned": (h, b) in TURNED or (h, b) in ON_GPSIMD,
                        "on_gpsimd": (h, b) in ON_GPSIMD,
                        "out": q_result[h][:, span, :].rearrange("p (b t) f -> p b (t f)", b=1),
                        "stores": [(q_view[:, h, span, :], q_result[h][:, span, :])],
                    }
                )
        keys_behind, first_queries = jobs[2:DUOS], jobs[DUOS : DUOS + 2 * UNIT_HEADS]
        jobs[2 : DUOS + 2 * UNIT_HEADS] = first_queries[0::2] + keys_behind + first_queries[1::2]
        flat = [(j, b) for j, job in enumerate(jobs) for b in range(len(job["banks"]))]
        sums_of = {}
        both_of = {}
        unfinished = []

        def start_bank(n):
            j, b = flat[n]
            heads, tiles = jobs[j]["banks"][b]
            if jobs[j].get("turned", False):
                sums_of[n] = project_turned(jobs[j]["unit"], heads[0], tiles)
            else:
                sums_of[n] = project(jobs[j]["unit"], heads, tiles)

        def rotate_bank(n, between=None, before_add=None):
            j, b = flat[n]
            job = jobs[j]
            heads, tiles = job["banks"][b]
            width = len(tiles) * HEAD
            if job.get("turned", False):
                both = rotate_turned(sums_of[n], tiles, job["on_gpsimd"])
                unfinished.append((n + (GPSIMD_DELAY if job["on_gpsimd"] else TURN_DELAY), both, tiles, job))
                return
            if b == 0:
                both_of[j] = products.tile([P, BANK // width, 2, width], F32, tag="both", name="both%d" % j)
            for place, h in enumerate(heads):
                multiply(sums_of[n], place * len(tiles), tiles, both_of[j][:, b * len(heads) + place, :, :])
                if place == 0 and between is not None:
                    between()
            if b == len(job["banks"]) - 1:
                used = len(job["banks"]) * len(heads)
                if before_add is not None:
                    before_add()
                job["adder"].tensor_tensor(
                    out=job["out"],
                    in0=both_of[j][:, 0:used, 0, :],
                    in1=both_of[j][:, 0:used, 1, :],
                    op=ADD,
                )
                for view, result in job["stores"]:
                    nc.sync.dma_start(out=view, in_=result)

        def finish_turned(n):
            for entry in [e for e in unfinished if e[0] <= n]:
                unfinished.remove(entry)
                both, tiles, job = entry[1:]
                turn_back(both, tiles, job["out"][:, 0, :])
                for view, result in job["stores"]:
                    nc.sync.dma_start(out=view, in_=result)

        def values(d):
            tiles = list(range(d * DUO, (d + 1) * DUO))
            sums = project(v_unit, list(range(UNIT_HEADS)), tiles)
            nc.scalar.copy(
                out=v_result[:, :, tiles[0] : tiles[0] + DUO, :].rearrange("p h t f -> p h (t f)"),
                in_=sums[:].rearrange("p (h m) -> p h m", h=UNIT_HEADS),
            )
            if d % 2 == 1:
                span = slice(tiles[0] - DUO, tiles[0] + DUO)
                nc.sync.dma_start(out=v_view[:, :, span, :], in_=v_result[:, :, span, :])

        turn_x(0)
        turn_x(1)
        for g in range(PASSES):
            keep_clock(k_rows[g][:, 0:2, :].rearrange("p j c -> p (j c)"), 1)
        group_weights(k_unit, nc.vector.tensor_copy)
        quantise_x(0)
        quantise_weights(k_unit)
        nc.vector.tensor_copy(out=factors[:, 1, 1, :, :], in_=factors[:, 0, 0, :, :])
        nc.vector.tensor_scalar(
            out=factors[:, 1, 0, :, :], in0=factors[:, 0, 1, :, :],
            scalar1=-1.0, scalar2=0.0, op0=MULT, op1=ADD,
        )
        turn_x(2)
        turn_x(3)
        start_bank(0)
        quantise_x(1)
        rotate_bank(0)
        start_bank(1)
        group_weights(q_units[0], nc.scalar.copy)
        turn_x(4)
        turn_x(5)
        keep_clock(x_rows[5][:, 0:BANK], 2)
        rotate_bank(1, before_add=lambda: quantise_weights(q_units[0]))
        start_bank(2)
        start_bank(3)
        turn_x(6)
        turn_x(7)
        turn_pairs()
        quantise_x(2)
        rotate_bank(2)
        start_bank(4)
        group_weights(q_units[1], nc.scalar.copy)
        rotate_bank(3)
        quantise_x(3)

        started = DUOS + 1
        quantised_units = 1
        for n in range(DUOS, len(flat)):
            if BACK_FIRST:
                finish_turned(n)
            while started <= min(n + LEAD, len(flat) - 1):
                start_bank(started)
                started += 1
            finish_turned(n)
            rotate_bank(n)
            ahead = min(n + LEAD + QUANT_AHEAD, len(flat) - 1)
            if quantised_units < Q_UNITS and jobs[flat[ahead][0]]["unit"] is q_units[quantised_units]:
                quantise_weights(q_units[quantised_units])
                quantised_units += 1
            if n == VALUE_QUANT_STEP:
                quantise_weights(v_unit)
            if n == DUOS:
                for a in range(2):
                    spread_pairs(a)
            if n in GROUP_STEPS:
                later, g = divmod(GROUP_STEPS.index(n), PASSES)
                group_pass((q_units + [v_unit])[GROUP_ORDER[later]], g, nc.scalar.copy)
            if n in VALUE_STEPS:
                values(VALUE_STEPS.index(n))
        finish_turned(len(flat) + GPSIMD_DELAY)
